import numpy as np
import ml_dtypes


def mxq(x, axis, fmt="e4m3"):
    dtype, down = {"e4m3": (ml_dtypes.float8_e4m3fn, 7), "e5m2": (ml_dtypes.float8_e5m2, 14)}[fmt]
    v = np.moveaxis(np.asarray(x, np.float32).astype(ml_dtypes.bfloat16).astype(np.float64), axis, -1)
    blocks = v.reshape(v.shape[:-1] + (-1, 32))
    amax = np.abs(blocks).max(-1, keepdims=True)
    byte = np.maximum(np.where(amax > 0, np.frexp(amax)[1] - 1 + 127, 0) - down, 1)
    scale = np.exp2(byte - 127.0)
    codes = (blocks / scale).astype(np.float32).astype(dtype).astype(np.float64)
    return np.moveaxis((codes * scale).reshape(v.shape), -1, axis)


WIDE = False


def mx_kscale(k):
    if not WIDE:
        return np.ones(k)
    levels = np.array([10, -10, 5, -5, 0])
    a = np.random.permutation(np.resize(levels, k // 512 * 4)).reshape(k // 512, 4)
    idx = np.arange(k)
    return np.exp2(a[idx // 512, idx % 128 // 32])


BF16 = ml_dtypes.bfloat16


def bf(x):
    return np.asarray(x, np.float32).astype(BF16)


def f64(x):
    return np.asarray(x).astype(np.float64)


E2M1 = np.array([0.0, 0.5, 1.0, 1.5, 2.0, 3.0, 4.0, 6.0, -0.0, -0.5, -1.0, -1.5, -2.0, -3.0, -4.0, -6.0])


def pack_weight(w, fmt):
    k, n = w.shape
    w = f64(bf(w)).reshape(k // 32, 32, n)
    amax = np.abs(w).max(1)
    if fmt == "e4m3":
        byte = np.frexp(amax)[1] - 1 + 127 - 7
    else:
        mant, ex = np.frexp(amax / 6.0)
        byte = np.where(mant > 0.5, ex, ex - 1) + 127
    byte = np.clip(np.where(amax > 0, byte, 1), 1, 254)
    scaled = (w * np.exp2(127.0 - byte)[:, None, :]).reshape(k, n).astype(np.float32)
    by_word = np.ascontiguousarray(scaled.reshape(k // 512, 128, 4, n).transpose(0, 1, 3, 2))
    if fmt == "e4m3":
        words = by_word.astype(ml_dtypes.float8_e4m3fn).view(np.uint8)
    else:
        c = by_word.astype(ml_dtypes.float4_e2m1fn).view(np.uint8) & 0xF
        words = c[..., 0::2] | (c[..., 1::2] << 4)
    return np.ascontiguousarray(words), np.ascontiguousarray(byte.astype(np.uint8).reshape(k // 512, 16, n))


def unpack_weight(words, scales, fmt):
    g, p, n, _ = words.shape
    if fmt == "e4m3":
        vals = np.ascontiguousarray(words).view(ml_dtypes.float8_e4m3fn).astype(np.float64)
    else:
        nib = np.empty((g, p, n, 4), np.uint8)
        nib[..., 0::2] = words & 0xF
        nib[..., 1::2] = words >> 4
        vals = E2M1[nib]
    vals = vals * np.repeat(np.exp2(scales.astype(np.float64) - 127.0), 8, axis=1)[..., None]
    return vals.transpose(0, 1, 3, 2).reshape(g * 512, n)


E, T, H, I = 4, 256, 1024, 1024
ALPHA = 1.702
LIMIT = 7.0
FMT = "e4m3"


def sigmoid(v):
    return 1.0 / (1.0 + np.exp(-v))


def apply_gate(gate_up):
    gate = gate_up[..., 0::2]
    up = gate_up[..., 1::2]
    gate = np.minimum(gate, LIMIT)
    up = np.clip(up, -LIMIT, LIMIT)
    glu = gate * sigmoid(gate * ALPHA)
    return (up + 1) * glu


def setup_inputs():
    s = mx_kscale(H)
    x = bf(np.random.standard_normal((E, T, H)) * s)
    gate_up_stack = np.random.standard_normal((E, H, 2 * I)) * 4.0 / np.sqrt(H) / s[:, None]
    gate_up_proj_bias = bf(np.random.standard_normal((E, 2 * I)) * 1.0)
    down_stack = np.random.standard_normal((E, I, H)) * 0.1 / np.sqrt(I)
    down_proj_bias = bf(np.random.standard_normal((E, H)) * 0.5)
    gate_up_proj_words, gate_up_proj_scales = pack_weight(gate_up_stack.reshape(-1, 2 * I), FMT)
    down_proj_words, down_proj_scales = pack_weight(down_stack.reshape(-1, H), FMT)
    return {"x": x,
            "gate_up_proj_words": gate_up_proj_words,
            "gate_up_proj_scales": gate_up_proj_scales,
            "gate_up_proj_bias": gate_up_proj_bias,
            "down_proj_words": down_proj_words,
            "down_proj_scales": down_proj_scales,
            "down_proj_bias": down_proj_bias}


def reference(x, gate_up_proj_words, gate_up_proj_scales, gate_up_proj_bias, down_proj_words, down_proj_scales, down_proj_bias):
    gate_up = (mxq(f64(x), 2, "e4m3") @ unpack_weight(gate_up_proj_words, gate_up_proj_scales, FMT).reshape(E, H, 2 * I)) + f64(gate_up_proj_bias)[:, None, :]
    h = apply_gate(gate_up)
    out = (mxq(h, 2, "e4m3") @ unpack_weight(down_proj_words, down_proj_scales, FMT).reshape(E, I, H)) + f64(down_proj_bias)[:, None, :]
    return out

@@ -1,0 +1,291 @@
+import math
+from contextlib import ExitStack
+
+import concourse.mybir as mybir
+from concourse.masks import make_identity
+
+F32 = mybir.dt.float32
+BF16 = mybir.dt.bfloat16
+I32 = mybir.dt.int32
+U32 = mybir.dt.uint32
+U8 = mybir.dt.uint8
+FP8X4 = mybir.dt.float8_e4m3fn_x4
+ALU = mybir.AluOpType
+ACT = mybir.ActivationFunctionType
+
+E, T, H, I = 4, 256, 1024, 1024
+P = 128
+K_PASS = 512
+BANK = 512
+TOKEN_TILES = T // P
+PASSES = H // K_PASS
+PLANES = 4
+LIMIT = 7.0
+ALPHA = 1.702
+GLU_AT_LIMIT = LIMIT / (1.0 + math.exp(-ALPHA * LIMIT))
+
+FLOPS = 2 * E * T * H * 2 * I + 2 * E * T * I * H
+
+
+def load_scale_planes(nc, planes, scales, first_group):
+    for quadrant in range(4):
+        nc.sync.dma_start(
+            out=planes[32 * quadrant : 32 * quadrant + 4 * PLANES, :].bitcast(I32),
+            in_=scales[
+                first_group : first_group + PLANES, 4 * quadrant : 4 * quadrant + 4, :
+            ].bitcast(I32),
+        )
+
+
+def tile_fakegptossexperts_e_kernel(
+    tc,
+    x,
+    gate_up_proj_words,
+    gate_up_proj_scales,
+    gate_up_proj_bias,
+    down_proj_words,
+    down_proj_scales,
+    down_proj_bias,
+    out,
+):
+    nc = tc.nc
+    groups = E * PASSES
+    units = [(e, m) for e in range(E) for m in range(TOKEN_TILES)]
+    with ExitStack() as ctx:
+        ctx.enter_context(tc.manual_schedule())
+        keep = ctx.enter_context(tc.tile_pool(name="keep", bufs=1))
+        per_expert = ctx.enter_context(tc.tile_pool(name="per_expert", bufs=2))
+        work = ctx.enter_context(tc.tile_pool(name="work", bufs=3))
+        per_unit = ctx.enter_context(tc.tile_pool(name="per_unit", bufs=2))
+        results = ctx.enter_context(tc.tile_pool(name="results", bufs=len(units)))
+        psum_gu = ctx.enter_context(tc.psum_pool(name="psum_gu", bufs=3))
+        psum_tr = ctx.enter_context(tc.psum_pool(name="psum_tr", bufs=3))
+        psum_out = ctx.enter_context(tc.psum_pool(name="psum_out", bufs=2))
+
+        x_sb = [keep.tile([P, TOKEN_TILES, H], BF16, name="x_sb%d" % e) for e in range(E)]
+        gu_words = [
+            keep.tile([P, 2 * I], U32, name="gu_words%d" % g, align_bytes=64) for g in range(groups)
+        ]
+        dn_words = [
+            keep.tile([P, H], U32, name="dn_words%d" % g, align_bytes=64) for g in range(groups)
+        ]
+        gu_planes = [
+            keep.tile([P, 2 * I], U8, name="gu_planes%d" % t, align_bytes=64)
+            for t in range(groups // PLANES)
+        ]
+        dn_planes = [
+            keep.tile([P, H], U8, name="dn_planes%d" % t, align_bytes=64)
+            for t in range(groups // PLANES)
+        ]
+        bias_rows = keep.tile([P, 2 * I + H], BF16, name="bias_rows")
+        pick_expert = keep.tile([P, E, P], BF16, name="pick_expert")
+        ident = keep.tile([P, P], F32, name="ident")
+
+        nc.vector.memset(gu_planes[0][:].bitcast(I32), 0)
+        nc.vector.memset(bias_rows[:].bitcast(I32), 0)
+        nc.vector.memset(pick_expert[:].bitcast(I32), 0)
+        for e in range(E):
+            nc.vector.memset(pick_expert[32 * e : 32 * e + 32, e, :], 1.0)
+        nc.vector.memset(dn_planes[0][:].bitcast(I32), 0)
+        nc.vector.memset(gu_planes[1][:].bitcast(I32), 0)
+        nc.vector.memset(dn_planes[1][:].bitcast(I32), 0)
+        make_identity(nc, ident[:])
+
+        def load_x(e):
+            nc.sync.dma_start(out=x_sb[e][:], in_=x[e].rearrange("(m p) h -> p m h", p=P))
+
+        def load_words(tiles, words, e, pieces):
+            width = tiles[0].shape[1] // pieces
+            for piece in range(pieces):
+                for g in range(PASSES * e, PASSES * e + PASSES):
+                    flat = words[g].rearrange("p n t -> p (n t)")
+                    nc.sync.dma_start(
+                        out=tiles[g][:, piece * width : (piece + 1) * width].bitcast(I32),
+                        in_=flat[:, 4 * piece * width : 4 * (piece + 1) * width].bitcast(I32),
+                    )
+
+        nc.scalar.dma_start(out=bias_rows[0:P:32, 0 : 2 * I], in_=gate_up_proj_bias)
+        nc.scalar.dma_start(out=bias_rows[0:P:32, 2 * I : 2 * I + H], in_=down_proj_bias)
+        load_x(0)
+        for e in range(E):
+            if e % 2 == 0:
+                load_scale_planes(nc, gu_planes[e // 2], gate_up_proj_scales, PASSES * e)
+            load_words(gu_words, gate_up_proj_words, e, 4 if e == 0 else 1)
+            if e + 1 < E:
+                load_x(e + 1)
+            if e % 2 == 0:
+                load_scale_planes(nc, dn_planes[e // 2], down_proj_scales, PASSES * e)
+            load_words(dn_words, down_proj_words, e, 1)
+
+        def plane_of(planes, group, cols):
+            offset = 4 * (group % PLANES)
+            return planes[group // PLANES][offset:P, cols]
+
+        bias_gu = {}
+        bias_dn = {}
+        x_mx = {}
+        h_sb = {}
+        h_mx = {}
+        sums = {}
+        glus = {}
+
+        def spread_gate_up_bias(e, bank):
+            if bank == 0:
+                bias_gu[e] = per_expert.tile([P, 2, I], F32, name="bias_gu")
+            spread = psum_tr.tile([P, BANK], F32, tag="tr", name="spread")
+            nc.tensor.matmul(
+                spread[:],
+                lhsT=pick_expert[:, e, :],
+                rhs=bias_rows[:, bank * BANK : (bank + 1) * BANK],
+                start=True,
+                stop=True,
+            )
+            pairs = spread[:].rearrange("p (i s) -> p s i", s=2)
+            cols = slice(bank * BANK // 2, (bank + 1) * BANK // 2)
+            nc.scalar.copy(out=bias_gu[e][:, 0, cols], in_=pairs[:, 0, :])
+            nc.scalar.activation(out=bias_gu[e][:, 1, cols], in_=pairs[:, 1, :], func=ACT.Copy, bias=1.0)
+
+        def spread_down_bias(e):
+            bias_dn[e] = per_expert.tile([P, H], BF16, name="bias_dn")
+            spread_dn = psum_tr.tile([P, H], BF16, tag="tr", name="spread_dn")
+            for b in range(H // BANK):
+                nc.tensor.matmul(
+                    spread_dn[:, b * BANK : (b + 1) * BANK],
+                    lhsT=pick_expert[:, e, :],
+                    rhs=bias_rows[:, 2 * I + b * BANK : 2 * I + (b + 1) * BANK],
+                    start=True,
+                    stop=True,
+                )
+            nc.scalar.copy(out=bias_dn[e][:], in_=spread_dn[:])
+
+        def transpose_words(rows, tag):
+            turned = psum_tr.tile([P, PASSES, 2, P], F32, tag="tr", name="turned")
+            words = rows.bitcast(F32)
+            for g in range(PASSES):
+                for u in range(2):
+                    nc.tensor.transpose(turned[:, g, u, :], words[:, 256 * g + u : 256 * (g + 1) : 2], ident[:])
+            grouped = per_unit.tile([P, PASSES, P, 4], BF16, name=tag + "_grouped", align_bytes=64)
+            nc.scalar.copy(out=grouped[:].bitcast(F32), in_=turned[:].rearrange("p g u r -> p g r u"))
+            codes = per_unit.tile([P, PASSES, P], U32, name=tag + "_codes", align_bytes=64)
+            scales = per_unit.tile([P, PASSES, P], U8, name=tag + "_scales", align_bytes=64)
+            return grouped, codes, scales
+
+        def quantise(mx):
+            grouped, codes, scales = mx
+            nc.vector.quantize_mx(
+                out=codes[:].rearrange("p g r -> p (g r)").bitcast(FP8X4),
+                scales=scales[:].rearrange("p g r -> p (g r)"),
+                in_=grouped[:].rearrange("p g r t -> p (g r t)"),
+            )
+
+        def multiply(acc, mx, words, planes, e, n_cols):
+            grouped, codes, scales = mx
+            for g in range(PASSES):
+                group = PASSES * e + g
+                nc.tensor.matmul_mx(
+                    out=acc[:],
+                    lhsT=codes[:, g, :].bitcast(FP8X4),
+                    lhsT_scale=scales[:, g, :],
+                    rhs=words[group][:, n_cols].bitcast(FP8X4),
+                    rhs_scale=plane_of(planes, group, n_cols),
+                    start=(g == 0),
+                    stop=(g == PASSES - 1),
+                )
+
+        def gate_up_bank(unit, bank):
+            e, m = unit
+            half, b = divmod(bank, 2)
+            if b == 0:
+                sums[(unit, half)] = work.tile([P, 2, K_PASS], F32, name="s")
+            gu = psum_gu.tile([P, BANK], F32, name="gu")
+            multiply(gu, x_mx[unit], gu_words, gu_planes, e, slice(bank * BANK, (bank + 1) * BANK))
+            nc.vector.tensor_tensor(
+                out=sums[(unit, half)][:, :, b * 256 : (b + 1) * 256].rearrange("p s i -> p i s"),
+                in0=gu[:].rearrange("p (i s) -> p i s", s=2),
+                in1=bias_gu[e][:, :, bank * 256 : (bank + 1) * 256].rearrange("p s i -> p i s"),
+                op=ALU.add,
+            )
+
+        def gate_function(unit, half):
+            glus[(unit, half)] = work.tile([P, K_PASS], F32, name="glu")
+            nc.scalar.activation(
+                out=glus[(unit, half)][:], in_=sums[(unit, half)][:, 0, :], func=ACT.Gelu_apprx_sigmoid
+            )
+
+        def clamp_up(unit, half):
+            up = sums[(unit, half)][:, 1, :]
+            nc.vector.tensor_scalar(
+                out=up, in0=up, scalar1=1.0 - LIMIT, scalar2=1.0 + LIMIT, op0=ALU.max, op1=ALU.min
+            )
+
+        def gated_product(unit, half):
+            if half == 0:
+                h_sb[unit] = per_unit.tile([P, I], BF16, name="h_sb")
+            nc.vector.scalar_tensor_tensor(
+                out=h_sb[unit][:, half * K_PASS : (half + 1) * K_PASS],
+                in0=glus[(unit, half)][:],
+                scalar=GLU_AT_LIMIT,
+                in1=sums[(unit, half)][:, 1, :],
+                op0=ALU.min,
+                op1=ALU.mult,
+            )
+
+        out_sb = {}
+
+        def down_bank(unit, b):
+            e, m = unit
+            if b == 0:
+                out_sb[unit] = results.tile([P, H], F32, name="out_sb")
+            n_cols = slice(b * BANK, (b + 1) * BANK)
+            acc = psum_out.tile([P, BANK], F32, name="acc")
+            multiply(acc, h_mx[unit], dn_words, dn_planes, e, n_cols)
+            nc.vector.tensor_tensor(out=out_sb[unit][:, n_cols], in0=acc[:], in1=bias_dn[e][:, n_cols], op=ALU.add)
+
+        def store(unit):
+            e, m = unit
+            nc.sync.dma_start(out=out[e, m * P : (m + 1) * P, :], in_=out_sb[unit][:])
+
+        x_mx[units[0]] = transpose_words(x_sb[0][:, 0, :], "x")
+        quantise(x_mx[units[0]])
+        for bank in range(2 * I // BANK):
+            spread_gate_up_bias(0, bank)
+        spread_down_bias(0)
+        for j, unit in enumerate(units):
+            e, m = unit
+            before = units[j - 1] if j > 0 else None
+            after = units[j + 1] if j + 1 < len(units) else None
+            gate_up_bank(unit, 0)
+            gate_up_bank(unit, 1)
+            if before:
+                h_mx[before] = transpose_words(h_sb[before][:], "h")
+            if after:
+                x_mx[after] = transpose_words(x_sb[after[0]][:, after[1], :], "x")
+            gate_function(unit, 0)
+            clamp_up(unit, 0)
+            if e + 1 < E:
+                spread_gate_up_bias(e + 1, 2 * m)
+            gate_up_bank(unit, 2)
+            if before:
+                quantise(h_mx[before])
+            if after:
+                quantise(x_mx[after])
+            gate_up_bank(unit, 3)
+            gate_function(unit, 1)
+            gated_product(unit, 0)
+            clamp_up(unit, 1)
+            if e + 1 < E:
+                spread_gate_up_bias(e + 1, 2 * m + 1)
+            if before:
+                down_bank(before, 0)
+            gated_product(unit, 1)
+            if before:
+                down_bank(before, 1)
+                store(before)
+            if m == TOKEN_TILES - 1 and e + 1 < E:
+                spread_down_bias(e + 1)
+        last = units[-1]
+        h_mx[last] = transpose_words(h_sb[last][:], "h")
+        quantise(h_mx[last])
+        for b in range(H // BANK):
+            down_bank(last, b)
+        store(last)

@@ -128,6 +128,7 @@ def tile_fakegptossexperts_e_kernel(
         h_mx = {}
         sums = {}
         glus = {}
+        ups = {}
 
         def spread_gate_up_bias(e, bank):
             if bank == 0:
@@ -158,12 +159,18 @@ def tile_fakegptossexperts_e_kernel(
                 )
             nc.scalar.copy(out=bias_dn[e][:], in_=spread_dn[:])
 
-        def transpose_words(rows, tag):
+        def alternate_words(g, u):
+            return slice(256 * g + u, 256 * (g + 1), 2)
+
+        def sorted_words(g, u):
+            return slice(256 * g + P * u, 256 * g + P * (u + 1))
+
+        def transpose_words(rows, word_cols, tag):
             turned = psum_tr.tile([P, PASSES, 2, P], F32, tag="tr", name="turned")
             words = rows.bitcast(F32)
             for g in range(PASSES):
                 for u in range(2):
-                    nc.tensor.transpose(turned[:, g, u, :], words[:, 256 * g + u : 256 * (g + 1) : 2], ident[:])
+                    nc.tensor.transpose(turned[:, g, u, :], words[:, word_cols(g, u)], ident[:])
             grouped = per_unit.tile([P, PASSES, P, 4], BF16, name=tag + "_grouped", align_bytes=64)
             nc.scalar.copy(out=grouped[:].bitcast(F32), in_=turned[:].rearrange("p g u r -> p g r u"))
             codes = per_unit.tile([P, PASSES, P], U32, name=tag + "_codes", align_bytes=64)
@@ -209,13 +216,20 @@ def tile_fakegptossexperts_e_kernel(
         def gate_function(unit, half):
             glus[(unit, half)] = work.tile([P, K_PASS], F32, name="glu")
             nc.scalar.activation(
-                out=glus[(unit, half)][:], in_=sums[(unit, half)][:, 0, :], func=ACT.Gelu_apprx_sigmoid
+                out=glus[(unit, half)][:].rearrange("q (u p c) -> q u p c", u=2, c=2),
+                in_=sums[(unit, half)][:, 0, :].rearrange("q (p u c) -> q u p c", u=2, c=2),
+                func=ACT.Gelu_apprx_sigmoid,
             )
 
         def clamp_up(unit, half):
-            up = sums[(unit, half)][:, 1, :]
-            nc.vector.tensor_scalar(
-                out=up, in0=up, scalar1=1.0 - LIMIT, scalar2=1.0 + LIMIT, op0=ALU.max, op1=ALU.min
+            ups[(unit, half)] = work.tile([P, K_PASS], F32, name="up")
+            nc.gpsimd.tensor_scalar(
+                out=ups[(unit, half)][:].rearrange("q (u p c) -> q u p c", u=2, c=2),
+                in0=sums[(unit, half)][:, 1, :].rearrange("q (p u c) -> q u p c", u=2, c=2),
+                scalar1=1.0 + LIMIT,
+                scalar2=1.0 - LIMIT,
+                op0=ALU.min,
+                op1=ALU.max,
             )
 
         def gated_product(unit, half):
@@ -225,7 +239,7 @@ def tile_fakegptossexperts_e_kernel(
                 out=h_sb[unit][:, half * K_PASS : (half + 1) * K_PASS],
                 in0=glus[(unit, half)][:],
                 scalar=GLU_AT_LIMIT,
-                in1=sums[(unit, half)][:, 1, :],
+                in1=ups[(unit, half)][:],
                 op0=ALU.min,
                 op1=ALU.mult,
             )
@@ -245,7 +259,7 @@ def tile_fakegptossexperts_e_kernel(
             e, m = unit
             nc.sync.dma_start(out=out[e, m * P : (m + 1) * P, :], in_=out_sb[unit][:])
 
-        x_mx[units[0]] = transpose_words(x_sb[0][:, 0, :], "x")
+        x_mx[units[0]] = transpose_words(x_sb[0][:, 0, :], alternate_words, "x")
         quantise(x_mx[units[0]])
         for bank in range(2 * I // BANK):
             spread_gate_up_bias(0, bank)
@@ -257,9 +271,9 @@ def tile_fakegptossexperts_e_kernel(
             gate_up_bank(unit, 0)
             gate_up_bank(unit, 1)
             if before:
-                h_mx[before] = transpose_words(h_sb[before][:], "h")
+                h_mx[before] = transpose_words(h_sb[before][:], sorted_words, "h")
             if after:
-                x_mx[after] = transpose_words(x_sb[after[0]][:, after[1], :], "x")
+                x_mx[after] = transpose_words(x_sb[after[0]][:, after[1], :], alternate_words, "x")
             gate_function(unit, 0)
             clamp_up(unit, 0)
             if e + 1 < E:
@@ -277,14 +291,13 @@ def tile_fakegptossexperts_e_kernel(
                 spread_gate_up_bias(e + 1, 2 * m + 1)
             if before:
                 down_bank(before, 0)
-            gated_product(unit, 1)
-            if before:
                 down_bank(before, 1)
                 store(before)
+            gated_product(unit, 1)
             if m == TOKEN_TILES - 1 and e + 1 < E:
                 spread_down_bias(e + 1)
         last = units[-1]
-        h_mx[last] = transpose_words(h_sb[last][:], "h")
+        h_mx[last] = transpose_words(h_sb[last][:], sorted_words, "h")
         quantise(h_mx[last])
         for b in range(H // BANK):
             down_bank(last, b)

@@ -57,9 +57,10 @@ def tile_fakegptossexperts_e_kernel(
         per_expert = ctx.enter_context(tc.tile_pool(name="per_expert", bufs=2))
         work = ctx.enter_context(tc.tile_pool(name="work", bufs=3))
         per_unit = ctx.enter_context(tc.tile_pool(name="per_unit", bufs=2))
+        small = ctx.enter_context(tc.tile_pool(name="small", bufs=3))
         results = ctx.enter_context(tc.tile_pool(name="results", bufs=len(units)))
-        psum_gu = ctx.enter_context(tc.psum_pool(name="psum_gu", bufs=3))
-        psum_tr = ctx.enter_context(tc.psum_pool(name="psum_tr", bufs=3))
+        psum_gu = ctx.enter_context(tc.psum_pool(name="psum_gu", bufs=4))
+        psum_tr = ctx.enter_context(tc.psum_pool(name="psum_tr", bufs=2))
         psum_out = ctx.enter_context(tc.psum_pool(name="psum_out", bufs=2))
 
         x_sb = [keep.tile([P, TOKEN_TILES, H], BF16, name="x_sb%d" % e) for e in range(E)]
@@ -111,11 +112,13 @@ def tile_fakegptossexperts_e_kernel(
             if e % 2 == 0:
                 load_scale_planes(nc, gu_planes[e // 2], gate_up_proj_scales, PASSES * e)
             load_words(gu_words, gate_up_proj_words, e, 4 if e == 0 else 1)
-            if e + 1 < E:
-                load_x(e + 1)
+            if e == 0:
+                load_x(1)
             if e % 2 == 0:
                 load_scale_planes(nc, dn_planes[e // 2], down_proj_scales, PASSES * e)
             load_words(dn_words, down_proj_words, e, 1)
+            if e + 2 < E:
+                load_x(e + 2)
 
         def plane_of(planes, group, cols):
             offset = 4 * (group % PLANES)
@@ -123,70 +126,79 @@ def tile_fakegptossexperts_e_kernel(
 
         bias_gu = {}
         bias_dn = {}
-        x_mx = {}
-        h_sb = {}
-        h_mx = {}
+        spreads = {}
+        turned = {}
+        grouped = {}
+        mx = {}
+        gus = {}
+        accs = {}
         sums = {}
         glus = {}
-        ups = {}
+        h_sb = {}
+        out_sb = {}
 
         def spread_gate_up_bias(e, bank):
-            if bank == 0:
-                bias_gu[e] = per_expert.tile([P, 2, I], F32, name="bias_gu")
-            spread = psum_tr.tile([P, BANK], F32, tag="tr", name="spread")
+            spreads[(e, bank)] = psum_tr.tile([P, BANK], F32, tag="tr", name="spread")
             nc.tensor.matmul(
-                spread[:],
+                spreads[(e, bank)][:],
                 lhsT=pick_expert[:, e, :],
                 rhs=bias_rows[:, bank * BANK : (bank + 1) * BANK],
                 start=True,
                 stop=True,
             )
-            pairs = spread[:].rearrange("p (i s) -> p s i", s=2)
+
+        def keep_gate_up_bias(e, bank):
+            if bank == 0:
+                bias_gu[e] = per_expert.tile([P, 2, I], F32, name="bias_gu")
+            pairs = spreads[(e, bank)][:].rearrange("p (i s) -> p s i", s=2)
             cols = slice(bank * BANK // 2, (bank + 1) * BANK // 2)
             nc.scalar.copy(out=bias_gu[e][:, 0, cols], in_=pairs[:, 0, :])
             nc.scalar.activation(out=bias_gu[e][:, 1, cols], in_=pairs[:, 1, :], func=ACT.Copy, bias=1.0)
 
         def spread_down_bias(e):
-            bias_dn[e] = per_expert.tile([P, H], BF16, name="bias_dn")
-            spread_dn = psum_tr.tile([P, H], BF16, tag="tr", name="spread_dn")
+            spreads[e] = psum_tr.tile([P, H], BF16, tag="tr", name="spread_dn")
             for b in range(H // BANK):
                 nc.tensor.matmul(
-                    spread_dn[:, b * BANK : (b + 1) * BANK],
+                    spreads[e][:, b * BANK : (b + 1) * BANK],
                     lhsT=pick_expert[:, e, :],
                     rhs=bias_rows[:, 2 * I + b * BANK : 2 * I + (b + 1) * BANK],
                     start=True,
                     stop=True,
                 )
-            nc.scalar.copy(out=bias_dn[e][:], in_=spread_dn[:])
 
-        def alternate_words(g, u):
-            return slice(256 * g + u, 256 * (g + 1), 2)
+        def keep_down_bias(e):
+            bias_dn[e] = per_expert.tile([P, H], BF16, name="bias_dn")
+            nc.scalar.copy(out=bias_dn[e][:], in_=spreads[e][:])
 
-        def sorted_words(g, u):
-            return slice(256 * g + P * u, 256 * g + P * (u + 1))
-
-        def transpose_words(rows, word_cols, tag):
-            turned = psum_tr.tile([P, PASSES, 2, P], F32, tag="tr", name="turned")
+        def transpose_words(what, unit):
+            rows = x_sb[unit[0]][:, unit[1], :] if what == "x" else h_sb[unit][:]
             words = rows.bitcast(F32)
+            turned[(what, unit)] = psum_tr.tile([P, PASSES, 2, P], F32, tag="tr", name="turned")
             for g in range(PASSES):
                 for u in range(2):
-                    nc.tensor.transpose(turned[:, g, u, :], words[:, word_cols(g, u)], ident[:])
-            grouped = per_unit.tile([P, PASSES, P, 4], BF16, name=tag + "_grouped", align_bytes=64)
-            nc.scalar.copy(out=grouped[:].bitcast(F32), in_=turned[:].rearrange("p g u r -> p g r u"))
-            codes = per_unit.tile([P, PASSES, P], U32, name=tag + "_codes", align_bytes=64)
-            scales = per_unit.tile([P, PASSES, P], U8, name=tag + "_scales", align_bytes=64)
-            return grouped, codes, scales
+                    nc.tensor.transpose(
+                        turned[(what, unit)][:, g, u, :], words[:, 256 * g + u : 256 * (g + 1) : 2], ident[:]
+                    )
 
-        def quantise(mx):
-            grouped, codes, scales = mx
+        def group_words(what, unit):
+            grouped[(what, unit)] = small.tile([P, PASSES, P, 4], BF16, name=what + "_grouped", align_bytes=64)
+            nc.scalar.copy(
+                out=grouped[(what, unit)][:].bitcast(F32),
+                in_=turned[(what, unit)][:].rearrange("p g u r -> p g r u"),
+            )
+
+        def quantise(what, unit):
+            codes = small.tile([P, PASSES, P], U32, name=what + "_codes", align_bytes=64)
+            scales = small.tile([P, PASSES, P], U8, name=what + "_scales", align_bytes=64)
             nc.vector.quantize_mx(
                 out=codes[:].rearrange("p g r -> p (g r)").bitcast(FP8X4),
                 scales=scales[:].rearrange("p g r -> p (g r)"),
-                in_=grouped[:].rearrange("p g r t -> p (g r t)"),
+                in_=grouped[(what, unit)][:].rearrange("p g r t -> p (g r t)"),
             )
+            mx[(what, unit)] = (codes, scales)
 
-        def multiply(acc, mx, words, planes, e, n_cols):
-            grouped, codes, scales = mx
+        def multiply(acc, codes_and_scales, words, planes, e, n_cols):
+            codes, scales = codes_and_scales
             for g in range(PASSES):
                 group = PASSES * e + g
                 nc.tensor.matmul_mx(
@@ -199,37 +211,32 @@ def tile_fakegptossexperts_e_kernel(
                     stop=(g == PASSES - 1),
                 )
 
-        def gate_up_bank(unit, bank):
-            e, m = unit
+        def gate_up_matmul(unit, bank):
+            gus[(unit, bank)] = psum_gu.tile([P, BANK], F32, name="gu")
+            n_cols = slice(bank * BANK, (bank + 1) * BANK)
+            multiply(gus[(unit, bank)], mx[("x", unit)], gu_words, gu_planes, unit[0], n_cols)
+
+        def add_gate_up_bias(unit, bank):
             half, b = divmod(bank, 2)
             if b == 0:
                 sums[(unit, half)] = work.tile([P, 2, K_PASS], F32, name="s")
-            gu = psum_gu.tile([P, BANK], F32, name="gu")
-            multiply(gu, x_mx[unit], gu_words, gu_planes, e, slice(bank * BANK, (bank + 1) * BANK))
             nc.vector.tensor_tensor(
                 out=sums[(unit, half)][:, :, b * 256 : (b + 1) * 256].rearrange("p s i -> p i s"),
-                in0=gu[:].rearrange("p (i s) -> p i s", s=2),
-                in1=bias_gu[e][:, :, bank * 256 : (bank + 1) * 256].rearrange("p s i -> p i s"),
+                in0=gus[(unit, bank)][:].rearrange("p (i s) -> p i s", s=2),
+                in1=bias_gu[unit[0]][:, :, bank * 256 : (bank + 1) * 256].rearrange("p s i -> p i s"),
                 op=ALU.add,
             )
 
         def gate_function(unit, half):
             glus[(unit, half)] = work.tile([P, K_PASS], F32, name="glu")
             nc.scalar.activation(
-                out=glus[(unit, half)][:].rearrange("q (u p c) -> q u p c", u=2, c=2),
-                in_=sums[(unit, half)][:, 0, :].rearrange("q (p u c) -> q u p c", u=2, c=2),
-                func=ACT.Gelu_apprx_sigmoid,
+                out=glus[(unit, half)][:], in_=sums[(unit, half)][:, 0, :], func=ACT.Gelu_apprx_sigmoid
             )
 
         def clamp_up(unit, half):
-            ups[(unit, half)] = work.tile([P, K_PASS], F32, name="up")
-            nc.gpsimd.tensor_scalar(
-                out=ups[(unit, half)][:].rearrange("q (u p c) -> q u p c", u=2, c=2),
-                in0=sums[(unit, half)][:, 1, :].rearrange("q (p u c) -> q u p c", u=2, c=2),
-                scalar1=1.0 + LIMIT,
-                scalar2=1.0 - LIMIT,
-                op0=ALU.min,
-                op1=ALU.max,
+            up = sums[(unit, half)][:, 1, :]
+            nc.vector.tensor_scalar(
+                out=up, in0=up, scalar1=1.0 - LIMIT, scalar2=1.0 + LIMIT, op0=ALU.max, op1=ALU.min
             )
 
         def gated_product(unit, half):
@@ -239,66 +246,98 @@ def tile_fakegptossexperts_e_kernel(
                 out=h_sb[unit][:, half * K_PASS : (half + 1) * K_PASS],
                 in0=glus[(unit, half)][:],
                 scalar=GLU_AT_LIMIT,
-                in1=ups[(unit, half)][:],
+                in1=sums[(unit, half)][:, 1, :],
                 op0=ALU.min,
                 op1=ALU.mult,
             )
 
-        out_sb = {}
+        def down_matmul(unit, b):
+            accs[(unit, b)] = psum_out.tile([P, BANK], F32, name="acc")
+            multiply(accs[(unit, b)], mx[("h", unit)], dn_words, dn_planes, unit[0], slice(b * BANK, (b + 1) * BANK))
 
-        def down_bank(unit, b):
+        def add_down_bias_and_store(unit, b):
             e, m = unit
             if b == 0:
                 out_sb[unit] = results.tile([P, H], F32, name="out_sb")
             n_cols = slice(b * BANK, (b + 1) * BANK)
-            acc = psum_out.tile([P, BANK], F32, name="acc")
-            multiply(acc, h_mx[unit], dn_words, dn_planes, e, n_cols)
-            nc.vector.tensor_tensor(out=out_sb[unit][:, n_cols], in0=acc[:], in1=bias_dn[e][:, n_cols], op=ALU.add)
+            nc.vector.tensor_tensor(
+                out=out_sb[unit][:, n_cols], in0=accs[(unit, b)][:], in1=bias_dn[e][:, n_cols], op=ALU.add
+            )
+            nc.sync.dma_start(out=out[e, m * P : (m + 1) * P, n_cols], in_=out_sb[unit][:, n_cols])
 
-        def store(unit):
-            e, m = unit
-            nc.sync.dma_start(out=out[e, m * P : (m + 1) * P, :], in_=out_sb[unit][:])
-
-        x_mx[units[0]] = transpose_words(x_sb[0][:, 0, :], alternate_words, "x")
-        quantise(x_mx[units[0]])
-        for bank in range(2 * I // BANK):
+        transpose_words("x", units[0])
+        group_words("x", units[0])
+        quantise("x", units[0])
+        for bank in range(2):
             spread_gate_up_bias(0, bank)
-        spread_down_bias(0)
-        for j, unit in enumerate(units):
-            e, m = unit
-            before = units[j - 1] if j > 0 else None
-            after = units[j + 1] if j + 1 < len(units) else None
-            gate_up_bank(unit, 0)
-            gate_up_bank(unit, 1)
-            if before:
-                h_mx[before] = transpose_words(h_sb[before][:], sorted_words, "h")
-            if after:
-                x_mx[after] = transpose_words(x_sb[after[0]][:, after[1], :], alternate_words, "x")
-            gate_function(unit, 0)
-            clamp_up(unit, 0)
-            if e + 1 < E:
+            keep_gate_up_bias(0, bank)
+        gate_up_matmul(units[0], 0)
+        for bank in range(2, 4):
+            spread_gate_up_bias(0, bank)
+            keep_gate_up_bias(0, bank)
+            gate_up_matmul(units[0], bank - 1)
+        transpose_words("x", units[1])
+        group_words("x", units[1])
+        gate_up_matmul(units[0], 3)
+
+        def unit_at(j):
+            return units[j] if 0 <= j < len(units) else None
+
+        for j in range(len(units) + 2):
+            unit = unit_at(j)
+            nxt = unit_at(j + 1)
+            second_next = unit_at(j + 2)
+            prev = unit_at(j - 1)
+            second_prev = unit_at(j - 2)
+            e, m = divmod(j, TOKEN_TILES)
+            bias_ahead = unit is not None and e + 1 < E
+            if prev:
+                transpose_words("h", prev)
+            if second_next:
+                transpose_words("x", second_next)
+            if second_prev:
+                down_matmul(second_prev, 0)
+                down_matmul(second_prev, 1)
+            if unit:
+                for bank in range(4):
+                    add_gate_up_bias(unit, bank)
+            if nxt:
+                quantise("x", nxt)
+            if unit:
+                clamp_up(unit, 0)
+                clamp_up(unit, 1)
+                gate_function(unit, 0)
+            if prev:
+                group_words("h", prev)
+            if unit:
+                gate_function(unit, 1)
+            if second_next:
+                group_words("x", second_next)
+            if unit:
+                gated_product(unit, 0)
+            if bias_ahead:
                 spread_gate_up_bias(e + 1, 2 * m)
-            gate_up_bank(unit, 2)
-            if before:
-                quantise(h_mx[before])
-            if after:
-                quantise(x_mx[after])
-            gate_up_bank(unit, 3)
-            gate_function(unit, 1)
-            gated_product(unit, 0)
-            clamp_up(unit, 1)
-            if e + 1 < E:
+            if nxt:
+                gate_up_matmul(nxt, 0)
+                gate_up_matmul(nxt, 1)
+            if second_prev:
+                add_down_bias_and_store(second_prev, 0)
+            if unit:
+                gated_product(unit, 1)
+            if prev:
+                quantise("h", prev)
+            if bias_ahead:
                 spread_gate_up_bias(e + 1, 2 * m + 1)
-            if before:
-                down_bank(before, 0)
-                down_bank(before, 1)
-                store(before)
-            gated_product(unit, 1)
-            if m == TOKEN_TILES - 1 and e + 1 < E:
-                spread_down_bias(e + 1)
-        last = units[-1]
-        h_mx[last] = transpose_words(h_sb[last][:], sorted_words, "h")
-        quantise(h_mx[last])
-        for b in range(H // BANK):
-            down_bank(last, b)
-        store(last)
+                keep_gate_up_bias(e + 1, 2 * m)
+            if nxt:
+                gate_up_matmul(nxt, 2)
+            if unit and m == 0:
+                spread_down_bias(e)
+            if bias_ahead:
+                keep_gate_up_bias(e + 1, 2 * m + 1)
+            if nxt:
+                gate_up_matmul(nxt, 3)
+            if unit and m == 0:
+                keep_down_bias(e)
+            if second_prev:
+                add_down_bias_and_store(second_prev, 1)

@@ -58,7 +58,7 @@ def tile_fakegptossexperts_e_kernel(
         work = ctx.enter_context(tc.tile_pool(name="work", bufs=3))
         per_unit = ctx.enter_context(tc.tile_pool(name="per_unit", bufs=2))
         small = ctx.enter_context(tc.tile_pool(name="small", bufs=3))
-        results = ctx.enter_context(tc.tile_pool(name="results", bufs=len(units)))
+        results = ctx.enter_context(tc.tile_pool(name="results", bufs=6))
         psum_gu = ctx.enter_context(tc.psum_pool(name="psum_gu", bufs=4))
         psum_tr = ctx.enter_context(tc.psum_pool(name="psum_tr", bufs=2))
         psum_out = ctx.enter_context(tc.psum_pool(name="psum_out", bufs=2))
@@ -107,18 +107,19 @@ def tile_fakegptossexperts_e_kernel(
 
         nc.scalar.dma_start(out=bias_rows[0:P:32, 0 : 2 * I], in_=gate_up_proj_bias)
         nc.scalar.dma_start(out=bias_rows[0:P:32, 2 * I : 2 * I + H], in_=down_proj_bias)
-        load_x(0)
-        for e in range(E):
+        def load_gate_up(e):
+            load_x(e)
             if e % 2 == 0:
                 load_scale_planes(nc, gu_planes[e // 2], gate_up_proj_scales, PASSES * e)
             load_words(gu_words, gate_up_proj_words, e, 4 if e == 0 else 1)
-            if e == 0:
-                load_x(1)
+
+        load_gate_up(0)
+        for e in range(E):
+            if e + 1 < E:
+                load_gate_up(e + 1)
             if e % 2 == 0:
                 load_scale_planes(nc, dn_planes[e // 2], down_proj_scales, PASSES * e)
             load_words(dn_words, down_proj_words, e, 1)
-            if e + 2 < E:
-                load_x(e + 2)
 
         def plane_of(planes, group, cols):
             offset = 4 * (group % PLANES)
@@ -134,6 +135,7 @@ def tile_fakegptossexperts_e_kernel(
         accs = {}
         sums = {}
         glus = {}
+        ups = {}
         h_sb = {}
         out_sb = {}
 
@@ -171,14 +173,14 @@ def tile_fakegptossexperts_e_kernel(
             nc.scalar.copy(out=bias_dn[e][:], in_=spreads[e][:])
 
         def transpose_words(what, unit):
-            rows = x_sb[unit[0]][:, unit[1], :] if what == "x" else h_sb[unit][:]
-            words = rows.bitcast(F32)
             turned[(what, unit)] = psum_tr.tile([P, PASSES, 2, P], F32, tag="tr", name="turned")
             for g in range(PASSES):
                 for u in range(2):
-                    nc.tensor.transpose(
-                        turned[(what, unit)][:, g, u, :], words[:, 256 * g + u : 256 * (g + 1) : 2], ident[:]
-                    )
+                    if what == "x":
+                        words = x_sb[unit[0]][:, unit[1], :].bitcast(F32)[:, 256 * g + u : 256 * (g + 1) : 2]
+                    else:
+                        words = h_sb[unit][:].bitcast(F32)[:, 256 * g + P * u : 256 * g + P * (u + 1)]
+                    nc.tensor.transpose(turned[(what, unit)][:, g, u, :], words, ident[:])
 
         def group_words(what, unit):
             grouped[(what, unit)] = small.tile([P, PASSES, P, 4], BF16, name=what + "_grouped", align_bytes=64)
@@ -228,25 +230,33 @@ def tile_fakegptossexperts_e_kernel(
             )
 
         def gate_function(unit, half):
-            glus[(unit, half)] = work.tile([P, K_PASS], F32, name="glu")
+            if half == 0:
+                glus[unit] = per_unit.tile([P, PASSES, K_PASS], F32, name="glu")
             nc.scalar.activation(
-                out=glus[(unit, half)][:], in_=sums[(unit, half)][:, 0, :], func=ACT.Gelu_apprx_sigmoid
+                out=glus[unit][:, half, :].rearrange("q (u p c) -> q u p c", u=2, c=2),
+                in_=sums[(unit, half)][:, 0, :].rearrange("q (p u c) -> q u p c", u=2, c=2),
+                func=ACT.Gelu_apprx_sigmoid,
             )
 
         def clamp_up(unit, half):
-            up = sums[(unit, half)][:, 1, :]
-            nc.vector.tensor_scalar(
-                out=up, in0=up, scalar1=1.0 - LIMIT, scalar2=1.0 + LIMIT, op0=ALU.max, op1=ALU.min
+            if half == 0:
+                ups[unit] = per_unit.tile([P, PASSES, K_PASS], F32, name="up")
+            nc.gpsimd.tensor_scalar(
+                out=ups[unit][:, half, :].rearrange("q (u p c) -> q u p c", u=2, c=2),
+                in0=sums[(unit, half)][:, 1, :].rearrange("q (p u c) -> q u p c", u=2, c=2),
+                scalar1=1.0 + LIMIT,
+                scalar2=1.0 - LIMIT,
+                op0=ALU.min,
+                op1=ALU.max,
             )
 
-        def gated_product(unit, half):
-            if half == 0:
-                h_sb[unit] = per_unit.tile([P, I], BF16, name="h_sb")
+        def gated_product(unit):
+            h_sb[unit] = per_unit.tile([P, I], BF16, name="h_sb")
             nc.vector.scalar_tensor_tensor(
-                out=h_sb[unit][:, half * K_PASS : (half + 1) * K_PASS],
-                in0=glus[(unit, half)][:],
+                out=h_sb[unit][:],
+                in0=glus[unit][:].rearrange("q g i -> q (g i)"),
                 scalar=GLU_AT_LIMIT,
-                in1=sums[(unit, half)][:, 1, :],
+                in1=ups[unit][:].rearrange("q g i -> q (g i)"),
                 op0=ALU.min,
                 op1=ALU.mult,
             )
@@ -291,52 +301,56 @@ def tile_fakegptossexperts_e_kernel(
             second_prev = unit_at(j - 2)
             e, m = divmod(j, TOKEN_TILES)
             bias_ahead = unit is not None and e + 1 < E
+            if unit:
+                add_gate_up_bias(unit, 0)
+                add_gate_up_bias(unit, 1)
+                clamp_up(unit, 0)
+            if prev:
+                gated_product(prev)
+            if second_prev:
+                down_matmul(second_prev, 0)
             if prev:
                 transpose_words("h", prev)
             if second_next:
                 transpose_words("x", second_next)
-            if second_prev:
-                down_matmul(second_prev, 0)
-                down_matmul(second_prev, 1)
             if unit:
-                for bank in range(4):
-                    add_gate_up_bias(unit, bank)
-            if nxt:
-                quantise("x", nxt)
-            if unit:
-                clamp_up(unit, 0)
-                clamp_up(unit, 1)
-                gate_function(unit, 0)
+                add_gate_up_bias(unit, 2)
             if prev:
                 group_words("h", prev)
             if unit:
-                gate_function(unit, 1)
+                add_gate_up_bias(unit, 3)
+                clamp_up(unit, 1)
+            if second_prev:
+                down_matmul(second_prev, 1)
+            if nxt:
+                quantise("x", nxt)
+            if unit:
+                gate_function(unit, 0)
             if second_next:
                 group_words("x", second_next)
-            if unit:
-                gated_product(unit, 0)
-            if bias_ahead:
-                spread_gate_up_bias(e + 1, 2 * m)
             if nxt:
                 gate_up_matmul(nxt, 0)
                 gate_up_matmul(nxt, 1)
-            if second_prev:
-                add_down_bias_and_store(second_prev, 0)
+            if bias_ahead:
+                spread_gate_up_bias(e + 1, 2 * m)
             if unit:
-                gated_product(unit, 1)
-            if prev:
-                quantise("h", prev)
+                gate_function(unit, 1)
             if bias_ahead:
                 spread_gate_up_bias(e + 1, 2 * m + 1)
-                keep_gate_up_bias(e + 1, 2 * m)
             if nxt:
                 gate_up_matmul(nxt, 2)
+            if bias_ahead:
+                keep_gate_up_bias(e + 1, 2 * m)
+            if nxt:
+                gate_up_matmul(nxt, 3)
+            if second_prev:
+                add_down_bias_and_store(second_prev, 0)
             if unit and m == 0:
                 spread_down_bias(e)
             if bias_ahead:
                 keep_gate_up_bias(e + 1, 2 * m + 1)
-            if nxt:
-                gate_up_matmul(nxt, 3)
+            if prev:
+                quantise("h", prev)
             if unit and m == 0:
                 keep_down_bias(e)
             if second_prev:

@@ -169,7 +169,7 @@ def tile_fakegptossexperts_e_kernel(
                 )
 
         def keep_down_bias(e):
-            bias_dn[e] = per_expert.tile([P, H], BF16, name="bias_dn")
+            bias_dn[e] = per_expert.tile([P, H], BF16, name="bias_dn", bufs=3)
             nc.scalar.copy(out=bias_dn[e][:], in_=spreads[e][:])
 
         def transpose_words(what, unit):
@@ -282,76 +282,74 @@ def tile_fakegptossexperts_e_kernel(
             spread_gate_up_bias(0, bank)
             keep_gate_up_bias(0, bank)
         gate_up_matmul(units[0], 0)
+        transpose_words("x", units[1])
+        group_words("x", units[1])
         for bank in range(2, 4):
             spread_gate_up_bias(0, bank)
             keep_gate_up_bias(0, bank)
             gate_up_matmul(units[0], bank - 1)
-        transpose_words("x", units[1])
-        group_words("x", units[1])
         gate_up_matmul(units[0], 3)
 
         def unit_at(j):
             return units[j] if 0 <= j < len(units) else None
 
-        for j in range(len(units) + 2):
-            unit = unit_at(j)
-            nxt = unit_at(j + 1)
-            second_next = unit_at(j + 2)
-            prev = unit_at(j - 1)
-            second_prev = unit_at(j - 2)
+        for j in range(len(units) + 3):
+            x_unit = unit_at(j + 2)
+            matmul_unit = unit_at(j + 1)
+            gate_unit = unit_at(j)
+            product_unit = unit_at(j - 1)
+            h_unit = unit_at(j - 2)
+            out_unit = unit_at(j - 3)
             e, m = divmod(j, TOKEN_TILES)
-            bias_ahead = unit is not None and e + 1 < E
-            if unit:
-                add_gate_up_bias(unit, 0)
-                add_gate_up_bias(unit, 1)
-                clamp_up(unit, 0)
-            if prev:
-                gated_product(prev)
-            if second_prev:
-                down_matmul(second_prev, 0)
-            if prev:
-                transpose_words("h", prev)
-            if second_next:
-                transpose_words("x", second_next)
-            if unit:
-                add_gate_up_bias(unit, 2)
-            if prev:
-                group_words("h", prev)
-            if unit:
-                add_gate_up_bias(unit, 3)
-                clamp_up(unit, 1)
-            if second_prev:
-                down_matmul(second_prev, 1)
-            if nxt:
-                quantise("x", nxt)
-            if unit:
-                gate_function(unit, 0)
-            if second_next:
-                group_words("x", second_next)
-            if nxt:
-                gate_up_matmul(nxt, 0)
-                gate_up_matmul(nxt, 1)
+            bias_ahead = gate_unit is not None and e + 1 < E
+            down_bias_now = gate_unit is not None and m == 0
+            if h_unit:
+                transpose_words("h", h_unit)
+            if x_unit:
+                transpose_words("x", x_unit)
+            if h_unit:
+                group_words("h", h_unit)
+            if out_unit:
+                down_matmul(out_unit, 0)
+                down_matmul(out_unit, 1)
+            if gate_unit:
+                add_gate_up_bias(gate_unit, 0)
+                add_gate_up_bias(gate_unit, 1)
+                clamp_up(gate_unit, 0)
+            if matmul_unit:
+                quantise("x", matmul_unit)
+                gate_up_matmul(matmul_unit, 0)
+            if gate_unit:
+                gate_function(gate_unit, 0)
+                add_gate_up_bias(gate_unit, 2)
+            if x_unit:
+                group_words("x", x_unit)
             if bias_ahead:
                 spread_gate_up_bias(e + 1, 2 * m)
-            if unit:
-                gate_function(unit, 1)
-            if bias_ahead:
-                spread_gate_up_bias(e + 1, 2 * m + 1)
-            if nxt:
-                gate_up_matmul(nxt, 2)
+            if product_unit:
+                gated_product(product_unit)
+            if gate_unit:
+                add_gate_up_bias(gate_unit, 3)
+                clamp_up(gate_unit, 1)
+            if h_unit:
+                quantise("h", h_unit)
+            if matmul_unit:
+                gate_up_matmul(matmul_unit, 1)
             if bias_ahead:
                 keep_gate_up_bias(e + 1, 2 * m)
-            if nxt:
-                gate_up_matmul(nxt, 3)
-            if second_prev:
-                add_down_bias_and_store(second_prev, 0)
-            if unit and m == 0:
+                spread_gate_up_bias(e + 1, 2 * m + 1)
+            if gate_unit:
+                gate_function(gate_unit, 1)
+            if matmul_unit:
+                gate_up_matmul(matmul_unit, 2)
+            if down_bias_now:
                 spread_down_bias(e)
+            if matmul_unit:
+                gate_up_matmul(matmul_unit, 3)
             if bias_ahead:
                 keep_gate_up_bias(e + 1, 2 * m + 1)
-            if prev:
-                quantise("h", prev)
-            if unit and m == 0:
+            if down_bias_now:
                 keep_down_bias(e)
-            if second_prev:
-                add_down_bias_and_store(second_prev, 1)
+            if out_unit:
+                add_down_bias_and_store(out_unit, 0)
+                add_down_bias_and_store(out_unit, 1)

@@ -221,9 +221,9 @@ def tile_fakegptossexperts_e_kernel(
         def add_gate_up_bias(unit, bank):
             half, b = divmod(bank, 2)
             if b == 0:
-                sums[(unit, half)] = work.tile([P, 2, K_PASS], F32, name="s")
+                sums[(unit, half)] = work.tile([P, K_PASS, 2], F32, name="s")
             nc.vector.tensor_tensor(
-                out=sums[(unit, half)][:, :, b * 256 : (b + 1) * 256].rearrange("p s i -> p i s"),
+                out=sums[(unit, half)][:, b * 256 : (b + 1) * 256, :],
                 in0=gus[(unit, bank)][:].rearrange("p (i s) -> p i s", s=2),
                 in1=bias_gu[unit[0]][:, :, bank * 256 : (bank + 1) * 256].rearrange("p s i -> p i s"),
                 op=ALU.add,
@@ -234,7 +234,7 @@ def tile_fakegptossexperts_e_kernel(
                 glus[unit] = per_unit.tile([P, PASSES, K_PASS], F32, name="glu")
             nc.scalar.activation(
                 out=glus[unit][:, half, :].rearrange("q (u p c) -> q u p c", u=2, c=2),
-                in_=sums[(unit, half)][:, 0, :].rearrange("q (p u c) -> q u p c", u=2, c=2),
+                in_=sums[(unit, half)][:, :, 0].rearrange("q (p u c) -> q u p c", u=2, c=2),
                 func=ACT.Gelu_apprx_sigmoid,
             )
 
@@ -243,7 +243,7 @@ def tile_fakegptossexperts_e_kernel(
                 ups[unit] = per_unit.tile([P, PASSES, K_PASS], F32, name="up")
             nc.gpsimd.tensor_scalar(
                 out=ups[unit][:, half, :].rearrange("q (u p c) -> q u p c", u=2, c=2),
-                in0=sums[(unit, half)][:, 1, :].rearrange("q (p u c) -> q u p c", u=2, c=2),
+                in0=sums[(unit, half)][:, :, 1].rearrange("q (p u c) -> q u p c", u=2, c=2),
                 scalar1=1.0 + LIMIT,
                 scalar2=1.0 - LIMIT,
                 op0=ALU.min,

@@ -20,6 +20,8 @@ BANK = 512
 TOKEN_TILES = T // P
 PASSES = H // K_PASS
 PLANES = 4
+SORTS = 8
+HALF = 2 * K_PASS
 LIMIT = 7.0
 ALPHA = 1.702
 GLU_AT_LIMIT = LIMIT / (1.0 + math.exp(-ALPHA * LIMIT))
@@ -50,112 +52,122 @@ def tile_fakegptossexperts_e_kernel(
 ):
     nc = tc.nc
     groups = E * PASSES
+    rounds = [(e, c) for e in range(E) for c in range(PASSES)]
     units = [(e, m) for e in range(E) for m in range(TOKEN_TILES)]
     with ExitStack() as ctx:
         ctx.enter_context(tc.manual_schedule())
         keep = ctx.enter_context(tc.tile_pool(name="keep", bufs=1))
+        sorted_pool = ctx.enter_context(tc.tile_pool(name="sorted_pool", bufs=6))
         per_expert = ctx.enter_context(tc.tile_pool(name="per_expert", bufs=2))
-        work = ctx.enter_context(tc.tile_pool(name="work", bufs=3))
-        per_unit = ctx.enter_context(tc.tile_pool(name="per_unit", bufs=2))
-        small = ctx.enter_context(tc.tile_pool(name="small", bufs=3))
-        results = ctx.enter_context(tc.tile_pool(name="results", bufs=6))
-        psum_gu = ctx.enter_context(tc.psum_pool(name="psum_gu", bufs=4))
+        per_round = ctx.enter_context(tc.tile_pool(name="per_round", bufs=2))
+        results = ctx.enter_context(tc.tile_pool(name="results", bufs=4))
+        psum_mx = ctx.enter_context(tc.psum_pool(name="psum_mx", bufs=6))
         psum_tr = ctx.enter_context(tc.psum_pool(name="psum_tr", bufs=2))
-        psum_out = ctx.enter_context(tc.psum_pool(name="psum_out", bufs=2))
 
         x_sb = [keep.tile([P, TOKEN_TILES, H], BF16, name="x_sb%d" % e) for e in range(E)]
-        gu_words = [
-            keep.tile([P, 2 * I], U32, name="gu_words%d" % g, align_bytes=64) for g in range(groups)
-        ]
-        dn_words = [
-            keep.tile([P, H], U32, name="dn_words%d" % g, align_bytes=64) for g in range(groups)
+        gu_raw = [keep.tile([P, 2 * I], U32, name="gu_raw%d" % g, align_bytes=64) for g in range(groups)]
+        dn_words = [keep.tile([P, H], U32, name="dn_words%d" % g, align_bytes=64) for g in range(groups)]
+        gu_planes_raw = [
+            keep.tile([P, 2 * I], U8, name="gu_planes_raw%d" % t, align_bytes=64) for t in range(groups // PLANES)
         ]
         gu_planes = [
-            keep.tile([P, 2 * I], U8, name="gu_planes%d" % t, align_bytes=64)
-            for t in range(groups // PLANES)
+            keep.tile([P, 2 * I], U8, name="gu_planes%d" % t, align_bytes=64) for t in range(groups // PLANES)
         ]
         dn_planes = [
-            keep.tile([P, H], U8, name="dn_planes%d" % t, align_bytes=64)
-            for t in range(groups // PLANES)
+            keep.tile([P, H], U8, name="dn_planes%d" % t, align_bytes=64) for t in range(groups // PLANES)
         ]
-        bias_rows = keep.tile([P, 2 * I + H], BF16, name="bias_rows")
+        bias_rows = keep.tile([P, H], BF16, name="bias_rows")
         pick_expert = keep.tile([P, E, P], BF16, name="pick_expert")
         ident = keep.tile([P, P], F32, name="ident")
+        bias_bf = keep.tile([P, E * PASSES, SORTS], BF16, name="bias_bf")
+        bias_gu = keep.tile([P, E * PASSES, SORTS // 2, 2], F32, name="bias_gu")
+        warm = keep.tile([P, 2], F32, name="warm")
 
-        nc.vector.memset(gu_planes[0][:].bitcast(I32), 0)
+        nc.vector.memset(warm[:], 0.0)
+        nc.vector.memset(gu_planes_raw[0][:].bitcast(I32), 0)
         nc.vector.memset(bias_rows[:].bitcast(I32), 0)
         nc.vector.memset(pick_expert[:].bitcast(I32), 0)
         for e in range(E):
             nc.vector.memset(pick_expert[32 * e : 32 * e + 32, e, :], 1.0)
+        nc.vector.memset(gu_planes_raw[1][:].bitcast(I32), 0)
         nc.vector.memset(dn_planes[0][:].bitcast(I32), 0)
-        nc.vector.memset(gu_planes[1][:].bitcast(I32), 0)
         nc.vector.memset(dn_planes[1][:].bitcast(I32), 0)
         make_identity(nc, ident[:])
+        nc.scalar.activation(out=warm[:, 1:2], in_=warm[:, 0:1], func=ACT.Gelu_apprx_sigmoid)
 
         def load_x(e):
-            nc.sync.dma_start(out=x_sb[e][:], in_=x[e].rearrange("(m p) h -> p m h", p=P))
+            for m in range(TOKEN_TILES):
+                nc.sync.dma_start(out=x_sb[e][:, m, :], in_=x[e, m * P : (m + 1) * P, :])
 
-        def load_words(tiles, words, e, pieces):
-            width = tiles[0].shape[1] // pieces
+        def load_words(tiles, words, g, pieces):
+            width = tiles[g].shape[1] // pieces
+            flat = words[g].rearrange("p n t -> p (n t)")
             for piece in range(pieces):
+                nc.sync.dma_start(
+                    out=tiles[g][:, piece * width : (piece + 1) * width].bitcast(I32),
+                    in_=flat[:, 4 * piece * width : 4 * (piece + 1) * width].bitcast(I32),
+                )
+
+        def load_gate_up_words(e):
+            for c in range(PASSES):
                 for g in range(PASSES * e, PASSES * e + PASSES):
-                    flat = words[g].rearrange("p n t -> p (n t)")
+                    flat = gate_up_proj_words[g].rearrange("p n t -> p (n t)")
                     nc.sync.dma_start(
-                        out=tiles[g][:, piece * width : (piece + 1) * width].bitcast(I32),
-                        in_=flat[:, 4 * piece * width : 4 * (piece + 1) * width].bitcast(I32),
+                        out=gu_raw[g][:, c * HALF : (c + 1) * HALF].bitcast(I32),
+                        in_=flat[:, 4 * c * HALF : 4 * (c + 1) * HALF].bitcast(I32),
                     )
 
-        nc.scalar.dma_start(out=bias_rows[0:P:32, 0 : 2 * I], in_=gate_up_proj_bias)
-        nc.scalar.dma_start(out=bias_rows[0:P:32, 2 * I : 2 * I + H], in_=down_proj_bias)
-        def load_gate_up(e):
-            load_x(e)
-            if e % 2 == 0:
-                load_scale_planes(nc, gu_planes[e // 2], gate_up_proj_scales, PASSES * e)
-            load_words(gu_words, gate_up_proj_words, e, 4 if e == 0 else 1)
+        def load_down_words(e):
+            for g in range(PASSES * e, PASSES * e + PASSES):
+                load_words(dn_words, down_proj_words, g, 1)
 
-        load_gate_up(0)
         for e in range(E):
-            if e + 1 < E:
-                load_gate_up(e + 1)
-            if e % 2 == 0:
-                load_scale_planes(nc, dn_planes[e // 2], down_proj_scales, PASSES * e)
-            load_words(dn_words, down_proj_words, e, 1)
+            nc.scalar.dma_start(
+                out=bias_bf[:, PASSES * e : PASSES * (e + 1), :],
+                in_=gate_up_proj_bias[e].rearrange("(c p j) -> p c j", c=PASSES, j=SORTS),
+            )
+        nc.scalar.dma_start(out=bias_rows[0:P:32, :], in_=down_proj_bias)
+
+        load_x(0)
+        load_scale_planes(nc, gu_planes_raw[0], gate_up_proj_scales, 0)
+        load_gate_up_words(0)
+        load_x(1)
+        load_gate_up_words(1)
+        load_scale_planes(nc, gu_planes_raw[1], gate_up_proj_scales, PLANES)
+        load_scale_planes(nc, dn_planes[0], down_proj_scales, 0)
+        load_down_words(0)
+        load_x(2)
+        load_gate_up_words(2)
+        load_down_words(1)
+        load_x(3)
+        load_gate_up_words(3)
+        load_scale_planes(nc, dn_planes[1], down_proj_scales, PLANES)
+        load_down_words(2)
+        load_down_words(3)
 
         def plane_of(planes, group, cols):
             offset = 4 * (group % PLANES)
             return planes[group // PLANES][offset:P, cols]
 
-        bias_gu = {}
         bias_dn = {}
         spreads = {}
         turned = {}
-        grouped = {}
-        mx = {}
+        x_grouped = {}
+        x_mx = {}
+        gu_sorted = {}
         gus = {}
-        accs = {}
-        sums = {}
         glus = {}
         ups = {}
-        h_sb = {}
+        clipped = {}
+        h_grouped = {}
+        h_mx = {}
+        accs = {}
         out_sb = {}
 
-        def spread_gate_up_bias(e, bank):
-            spreads[(e, bank)] = psum_tr.tile([P, BANK], F32, tag="tr", name="spread")
-            nc.tensor.matmul(
-                spreads[(e, bank)][:],
-                lhsT=pick_expert[:, e, :],
-                rhs=bias_rows[:, bank * BANK : (bank + 1) * BANK],
-                start=True,
-                stop=True,
-            )
-
-        def keep_gate_up_bias(e, bank):
-            if bank == 0:
-                bias_gu[e] = per_expert.tile([P, 2, I], F32, name="bias_gu")
-            pairs = spreads[(e, bank)][:].rearrange("p (i s) -> p s i", s=2)
-            cols = slice(bank * BANK // 2, (bank + 1) * BANK // 2)
-            nc.scalar.copy(out=bias_gu[e][:, 0, cols], in_=pairs[:, 0, :])
-            nc.scalar.activation(out=bias_gu[e][:, 1, cols], in_=pairs[:, 1, :], func=ACT.Copy, bias=1.0)
+        def prepare_gate_up_bias():
+            pairs = bias_bf[:].rearrange("p k (t s) -> p k t s", s=2)
+            nc.scalar.copy(out=bias_gu[:, :, :, 0], in_=pairs[:, :, :, 0])
+            nc.scalar.activation(out=bias_gu[:, :, :, 1], in_=pairs[:, :, :, 1], func=ACT.Copy, bias=1.0)
 
         def spread_down_bias(e):
             spreads[e] = psum_tr.tile([P, H], BF16, tag="tr", name="spread_dn")
@@ -163,7 +175,7 @@ def tile_fakegptossexperts_e_kernel(
                 nc.tensor.matmul(
                     spreads[e][:, b * BANK : (b + 1) * BANK],
                     lhsT=pick_expert[:, e, :],
-                    rhs=bias_rows[:, 2 * I + b * BANK : 2 * I + (b + 1) * BANK],
+                    rhs=bias_rows[:, b * BANK : (b + 1) * BANK],
                     start=True,
                     stop=True,
                 )
@@ -172,98 +184,130 @@ def tile_fakegptossexperts_e_kernel(
             bias_dn[e] = per_expert.tile([P, H], BF16, name="bias_dn", bufs=3)
             nc.scalar.copy(out=bias_dn[e][:], in_=spreads[e][:])
 
-        def transpose_words(what, unit):
-            turned[(what, unit)] = psum_tr.tile([P, PASSES, 2, P], F32, tag="tr", name="turned")
+        def transpose_x(unit):
+            e, m = unit
+            turned[unit] = psum_tr.tile([P, PASSES, 2, P], F32, tag="tr", name="turned")
             for g in range(PASSES):
                 for u in range(2):
-                    if what == "x":
-                        words = x_sb[unit[0]][:, unit[1], :].bitcast(F32)[:, 256 * g + u : 256 * (g + 1) : 2]
-                    else:
-                        words = h_sb[unit][:].bitcast(F32)[:, 256 * g + P * u : 256 * g + P * (u + 1)]
-                    nc.tensor.transpose(turned[(what, unit)][:, g, u, :], words, ident[:])
+                    words = x_sb[e][:, m, :].bitcast(F32)[:, 256 * g + u : 256 * (g + 1) : 2]
+                    nc.tensor.transpose(turned[unit][:, g, u, :], words, ident[:])
 
-        def group_words(what, unit):
-            grouped[(what, unit)] = small.tile([P, PASSES, P, 4], BF16, name=what + "_grouped", align_bytes=64)
+        def group_x(unit):
+            e, m = unit
+            if m == 0:
+                x_grouped[e] = per_expert.tile([P, PASSES, T, 4], BF16, name="x_grouped", align_bytes=64)
             nc.scalar.copy(
-                out=grouped[(what, unit)][:].bitcast(F32),
-                in_=turned[(what, unit)][:].rearrange("p g u r -> p g r u"),
+                out=x_grouped[e][:].bitcast(F32)[:, :, m * P : (m + 1) * P, :],
+                in_=turned[unit][:].rearrange("p g u r -> p g r u"),
             )
 
-        def quantise(what, unit):
-            codes = small.tile([P, PASSES, P], U32, name=what + "_codes", align_bytes=64)
-            scales = small.tile([P, PASSES, P], U8, name=what + "_scales", align_bytes=64)
+        def quantise_x(e):
+            codes = per_expert.tile([P, PASSES, T], U32, name="x_codes", align_bytes=64)
+            scales = per_expert.tile([P, PASSES, T], U8, name="x_scales", align_bytes=64)
             nc.vector.quantize_mx(
                 out=codes[:].rearrange("p g r -> p (g r)").bitcast(FP8X4),
                 scales=scales[:].rearrange("p g r -> p (g r)"),
-                in_=grouped[(what, unit)][:].rearrange("p g r t -> p (g r t)"),
+                in_=x_grouped[e][:].rearrange("p g r t -> p (g r t)"),
             )
-            mx[(what, unit)] = (codes, scales)
+            x_mx[e] = (codes, scales)
 
-        def multiply(acc, codes_and_scales, words, planes, e, n_cols):
-            codes, scales = codes_and_scales
-            for g in range(PASSES):
-                group = PASSES * e + g
-                nc.tensor.matmul_mx(
-                    out=acc[:],
-                    lhsT=codes[:, g, :].bitcast(FP8X4),
-                    lhsT_scale=scales[:, g, :],
-                    rhs=words[group][:, n_cols].bitcast(FP8X4),
-                    rhs_scale=plane_of(planes, group, n_cols),
-                    start=(g == 0),
-                    stop=(g == PASSES - 1),
-                )
-
-        def gate_up_matmul(unit, bank):
-            gus[(unit, bank)] = psum_gu.tile([P, BANK], F32, name="gu")
-            n_cols = slice(bank * BANK, (bank + 1) * BANK)
-            multiply(gus[(unit, bank)], mx[("x", unit)], gu_words, gu_planes, unit[0], n_cols)
-
-        def add_gate_up_bias(unit, bank):
-            half, b = divmod(bank, 2)
-            if b == 0:
-                sums[(unit, half)] = work.tile([P, K_PASS, 2], F32, name="s")
-            nc.vector.tensor_tensor(
-                out=sums[(unit, half)][:, b * 256 : (b + 1) * 256, :],
-                in0=gus[(unit, bank)][:].rearrange("p (i s) -> p i s", s=2),
-                in1=bias_gu[unit[0]][:, :, bank * 256 : (bank + 1) * 256].rearrange("p s i -> p i s"),
-                op=ALU.add,
+        def sort_planes(t):
+            nc.vector.tensor_copy(
+                out=gu_planes[t][:].rearrange("q (c j p) -> q c j p", c=PASSES, j=SORTS),
+                in_=gu_planes_raw[t][:].rearrange("q (c p j) -> q c j p", c=PASSES, j=SORTS),
             )
 
-        def gate_function(unit, half):
-            if half == 0:
-                glus[unit] = per_unit.tile([P, PASSES, K_PASS], F32, name="glu")
+        def sort_words(rnd, g):
+            e, c = rnd
+            gu_sorted[(rnd, g)] = sorted_pool.tile([P, SORTS, P], U32, name="gu_sorted", align_bytes=64)
+            nc.vector.tensor_copy(
+                out=gu_sorted[(rnd, g)][:].bitcast(I32),
+                in_=gu_raw[PASSES * e + g][:, c * HALF : (c + 1) * HALF].bitcast(I32).rearrange(
+                    "q (p j) -> q j p", j=SORTS
+                ),
+            )
+
+        def gate_up_matmul(rnd, t):
+            e, c = rnd
+            codes, scales = x_mx[e]
+            gus[(rnd, t)] = psum_mx.tile([P, 2, T], F32, tag="bank", name="gu")
+            for s in range(2):
+                j = 2 * t + s
+                cols = slice(c * HALF + j * P, c * HALF + (j + 1) * P)
+                for g in range(PASSES):
+                    nc.tensor.matmul_mx(
+                        out=gus[(rnd, t)][:, s, :],
+                        lhsT=gu_sorted[(rnd, g)][:, j, :].bitcast(FP8X4),
+                        lhsT_scale=plane_of(gu_planes, PASSES * e + g, cols),
+                        rhs=codes[:, g, :].bitcast(FP8X4),
+                        rhs_scale=scales[:, g, :],
+                        start=(g == 0),
+                        stop=(g == PASSES - 1),
+                    )
+
+        def leave_psum(rnd, t):
+            e, c = rnd
+            if t == 0:
+                glus[rnd] = per_round.tile([P, 4, T], F32, name="glu", bufs=3)
+                ups[rnd] = per_round.tile([P, 4, T], F32, name="up", bufs=3)
+            k = PASSES * e + c
             nc.scalar.activation(
-                out=glus[unit][:, half, :].rearrange("q (u p c) -> q u p c", u=2, c=2),
-                in_=sums[(unit, half)][:, :, 0].rearrange("q (p u c) -> q u p c", u=2, c=2),
-                func=ACT.Gelu_apprx_sigmoid,
+                out=glus[rnd][:, t, :], in_=gus[(rnd, t)][:, 0, :], func=ACT.Gelu_apprx_sigmoid,
+                bias=bias_gu[:, k, t, 0:1],
+            )
+            nc.scalar.activation(
+                out=ups[rnd][:, t, :], in_=gus[(rnd, t)][:, 1, :], func=ACT.Identity, bias=bias_gu[:, k, t, 1:2]
             )
 
-        def clamp_up(unit, half):
-            if half == 0:
-                ups[unit] = per_unit.tile([P, PASSES, K_PASS], F32, name="up")
-            nc.gpsimd.tensor_scalar(
-                out=ups[unit][:, half, :].rearrange("q (u p c) -> q u p c", u=2, c=2),
-                in0=sums[(unit, half)][:, :, 1].rearrange("q (p u c) -> q u p c", u=2, c=2),
+        def clamp_up(rnd):
+            clipped[rnd] = per_round.tile([P, T, 4], F32, name="clipped")
+            nc.vector.tensor_scalar(
+                out=clipped[rnd][:],
+                in0=ups[rnd][:].rearrange("q t r -> q r t"),
                 scalar1=1.0 + LIMIT,
                 scalar2=1.0 - LIMIT,
                 op0=ALU.min,
                 op1=ALU.max,
             )
 
-        def gated_product(unit):
-            h_sb[unit] = per_unit.tile([P, I], BF16, name="h_sb")
+        def gated_product(rnd):
+            h_grouped[rnd] = per_round.tile([P, T, 4], BF16, name="h_grouped", align_bytes=64)
             nc.vector.scalar_tensor_tensor(
-                out=h_sb[unit][:],
-                in0=glus[unit][:].rearrange("q g i -> q (g i)"),
+                out=h_grouped[rnd][:],
+                in0=glus[rnd][:].rearrange("q t r -> q r t"),
                 scalar=GLU_AT_LIMIT,
-                in1=ups[unit][:].rearrange("q g i -> q (g i)"),
+                in1=clipped[rnd][:],
                 op0=ALU.min,
                 op1=ALU.mult,
             )
 
+        def quantise_h(rnd):
+            codes = per_round.tile([P, T], U32, name="h_codes", align_bytes=64, bufs=4)
+            scales = per_round.tile([P, T], U8, name="h_scales", align_bytes=64, bufs=4)
+            nc.vector.quantize_mx(
+                out=codes[:].bitcast(FP8X4),
+                scales=scales[:],
+                in_=h_grouped[rnd][:].rearrange("p r t -> p (r t)"),
+            )
+            h_mx[rnd] = (codes, scales)
+
         def down_matmul(unit, b):
-            accs[(unit, b)] = psum_out.tile([P, BANK], F32, name="acc")
-            multiply(accs[(unit, b)], mx[("h", unit)], dn_words, dn_planes, unit[0], slice(b * BANK, (b + 1) * BANK))
+            e, m = unit
+            accs[(unit, b)] = psum_mx.tile([P, BANK], F32, tag="bank", name="acc")
+            n_cols = slice(b * BANK, (b + 1) * BANK)
+            tokens = slice(m * P, (m + 1) * P)
+            for c in range(PASSES):
+                codes, scales = h_mx[(e, c)]
+                group = PASSES * e + c
+                nc.tensor.matmul_mx(
+                    out=accs[(unit, b)][:],
+                    lhsT=codes[:, tokens].bitcast(FP8X4),
+                    lhsT_scale=scales[:, tokens],
+                    rhs=dn_words[group][:, n_cols].bitcast(FP8X4),
+                    rhs_scale=plane_of(dn_planes, group, n_cols),
+                    start=(c == 0),
+                    stop=(c == PASSES - 1),
+                )
 
         def add_down_bias_and_store(unit, b):
             e, m = unit
@@ -275,81 +319,54 @@ def tile_fakegptossexperts_e_kernel(
             )
             nc.sync.dma_start(out=out[e, m * P : (m + 1) * P, n_cols], in_=out_sb[unit][:, n_cols])
 
-        transpose_words("x", units[0])
-        group_words("x", units[0])
-        quantise("x", units[0])
-        for bank in range(2):
-            spread_gate_up_bias(0, bank)
-            keep_gate_up_bias(0, bank)
-        gate_up_matmul(units[0], 0)
-        transpose_words("x", units[1])
-        group_words("x", units[1])
-        for bank in range(2, 4):
-            spread_gate_up_bias(0, bank)
-            keep_gate_up_bias(0, bank)
-            gate_up_matmul(units[0], bank - 1)
-        gate_up_matmul(units[0], 3)
+        prepare_gate_up_bias()
+        for m in range(TOKEN_TILES):
+            transpose_x((0, m))
+            group_x((0, m))
+        sort_planes(0)
+        sort_words(rounds[0], 0)
+        quantise_x(0)
+        sort_words(rounds[0], 1)
 
-        def unit_at(j):
-            return units[j] if 0 <= j < len(units) else None
-
-        for j in range(len(units) + 3):
-            x_unit = unit_at(j + 2)
-            matmul_unit = unit_at(j + 1)
-            gate_unit = unit_at(j)
-            product_unit = unit_at(j - 1)
-            h_unit = unit_at(j - 2)
-            out_unit = unit_at(j - 3)
-            e, m = divmod(j, TOKEN_TILES)
-            bias_ahead = gate_unit is not None and e + 1 < E
-            down_bias_now = gate_unit is not None and m == 0
-            if h_unit:
-                transpose_words("h", h_unit)
-            if x_unit:
-                transpose_words("x", x_unit)
-            if h_unit:
-                group_words("h", h_unit)
+        for i in range(len(rounds) + 3):
+            rnd = rounds[i] if i < len(rounds) else None
+            ahead = rounds[i + 1] if i + 1 < len(rounds) else None
+            behind = rounds[i - 1] if 1 <= i <= len(rounds) else None
+            out_unit = units[i - 3] if 0 <= i - 3 < len(units) else None
+            e, c = divmod(i, PASSES)
+            next_x = e + 1 if rnd and e + 1 < E else None
+            if behind:
+                clamp_up(behind)
+            if rnd:
+                for t in range(2):
+                    gate_up_matmul(rnd, t)
+                    leave_psum(rnd, t)
+            if ahead:
+                sort_words(ahead, 0)
+            if behind:
+                gated_product(behind)
+            if ahead:
+                sort_words(ahead, 1)
+            if behind:
+                quantise_h(behind)
+            if next_x and c == 1:
+                quantise_x(next_x)
+            if rnd:
+                for t in range(2, 4):
+                    gate_up_matmul(rnd, t)
+                    leave_psum(rnd, t)
             if out_unit:
                 down_matmul(out_unit, 0)
                 down_matmul(out_unit, 1)
-            if gate_unit:
-                add_gate_up_bias(gate_unit, 0)
-                add_gate_up_bias(gate_unit, 1)
-                clamp_up(gate_unit, 0)
-            if matmul_unit:
-                quantise("x", matmul_unit)
-                gate_up_matmul(matmul_unit, 0)
-            if gate_unit:
-                gate_function(gate_unit, 0)
-                add_gate_up_bias(gate_unit, 2)
-            if x_unit:
-                group_words("x", x_unit)
-            if bias_ahead:
-                spread_gate_up_bias(e + 1, 2 * m)
-            if product_unit:
-                gated_product(product_unit)
-            if gate_unit:
-                add_gate_up_bias(gate_unit, 3)
-                clamp_up(gate_unit, 1)
-            if h_unit:
-                quantise("h", h_unit)
-            if matmul_unit:
-                gate_up_matmul(matmul_unit, 1)
-            if bias_ahead:
-                keep_gate_up_bias(e + 1, 2 * m)
-                spread_gate_up_bias(e + 1, 2 * m + 1)
-            if gate_unit:
-                gate_function(gate_unit, 1)
-            if matmul_unit:
-                gate_up_matmul(matmul_unit, 2)
-            if down_bias_now:
+            if next_x and c == 0:
+                for m in range(TOKEN_TILES):
+                    transpose_x((next_x, m))
+                    group_x((next_x, m))
+            if rnd and c == 0:
                 spread_down_bias(e)
-            if matmul_unit:
-                gate_up_matmul(matmul_unit, 3)
-            if bias_ahead:
-                keep_gate_up_bias(e + 1, 2 * m + 1)
-            if down_bias_now:
                 keep_down_bias(e)
             if out_unit:
                 add_down_bias_and_store(out_unit, 0)
                 add_down_bias_and_store(out_unit, 1)
+            if i == 2:
+                sort_planes(1)

@@ -211,19 +211,20 @@ def tile_fakegptossexperts_e_kernel(
             )
             x_mx[e] = (codes, scales)
 
-        def sort_planes(t):
+        def sort_planes(t, c):
+            cols = slice(c * HALF, (c + 1) * HALF)
             nc.vector.tensor_copy(
-                out=gu_planes[t][:].rearrange("q (c j p) -> q c j p", c=PASSES, j=SORTS),
-                in_=gu_planes_raw[t][:].rearrange("q (c p j) -> q c j p", c=PASSES, j=SORTS),
+                out=gu_planes[t][:, cols].rearrange("q (a i p) -> q a p i", a=SORTS // 4, i=4),
+                in_=gu_planes_raw[t][:, cols].rearrange("q (p a i) -> q a p i", a=SORTS // 4, i=4),
             )
 
         def sort_words(rnd, g):
             e, c = rnd
             gu_sorted[(rnd, g)] = sorted_pool.tile([P, SORTS, P], U32, name="gu_sorted", align_bytes=64)
             nc.vector.tensor_copy(
-                out=gu_sorted[(rnd, g)][:].bitcast(I32),
+                out=gu_sorted[(rnd, g)][:].bitcast(I32).rearrange("q (a i) p -> q a p i", i=4),
                 in_=gu_raw[PASSES * e + g][:, c * HALF : (c + 1) * HALF].bitcast(I32).rearrange(
-                    "q (p j) -> q j p", j=SORTS
+                    "q (p a i) -> q a p i", a=SORTS // 4, i=4
                 ),
             )
 
@@ -262,8 +263,8 @@ def tile_fakegptossexperts_e_kernel(
         def clamp_up(rnd):
             clipped[rnd] = per_round.tile([P, T, 4], F32, name="clipped")
             nc.vector.tensor_scalar(
-                out=clipped[rnd][:],
-                in0=ups[rnd][:].rearrange("q t r -> q r t"),
+                out=clipped[rnd][:].rearrange("q (b i) t -> q b t i", i=4),
+                in0=ups[rnd][:].rearrange("q t (b i) -> q b t i", i=4),
                 scalar1=1.0 + LIMIT,
                 scalar2=1.0 - LIMIT,
                 op0=ALU.min,
@@ -323,10 +324,11 @@ def tile_fakegptossexperts_e_kernel(
         for m in range(TOKEN_TILES):
             transpose_x((0, m))
             group_x((0, m))
-        sort_planes(0)
+        sort_planes(0, 0)
         sort_words(rounds[0], 0)
         quantise_x(0)
         sort_words(rounds[0], 1)
+        sort_planes(0, 1)
 
         for i in range(len(rounds) + 3):
             rnd = rounds[i] if i < len(rounds) else None
@@ -369,4 +371,5 @@ def tile_fakegptossexperts_e_kernel(
                 add_down_bias_and_store(out_unit, 0)
                 add_down_bias_and_store(out_unit, 1)
             if i == 2:
-                sort_planes(1)
+                sort_planes(1, 0)
+                sort_planes(1, 1)

@@ -79,11 +79,13 @@ def tile_fakegptossexperts_e_kernel(
         bias_rows = keep.tile([P, H], BF16, name="bias_rows")
         pick_expert = keep.tile([P, E, P], BF16, name="pick_expert")
         ident = keep.tile([P, P], F32, name="ident")
-        bias_bf = keep.tile([P, E * PASSES, SORTS], BF16, name="bias_bf")
+        bias_src = keep.tile([P, HALF], BF16, name="bias_src")
+        ident_bf = keep.tile([P, P], BF16, name="ident_bf")
         bias_gu = keep.tile([P, E * PASSES, SORTS // 2, 2], F32, name="bias_gu")
         warm = keep.tile([P, 2], F32, name="warm")
 
         nc.vector.memset(warm[:], 0.0)
+        nc.vector.memset(bias_src[:].bitcast(I32), 0)
         nc.vector.memset(gu_planes_raw[0][:].bitcast(I32), 0)
         nc.vector.memset(bias_rows[:].bitcast(I32), 0)
         nc.vector.memset(pick_expert[:].bitcast(I32), 0)
@@ -93,6 +95,7 @@ def tile_fakegptossexperts_e_kernel(
         nc.vector.memset(dn_planes[0][:].bitcast(I32), 0)
         nc.vector.memset(dn_planes[1][:].bitcast(I32), 0)
         make_identity(nc, ident[:])
+        make_identity(nc, ident_bf[:])
         nc.scalar.activation(out=warm[:, 1:2], in_=warm[:, 0:1], func=ACT.Gelu_apprx_sigmoid)
 
         def load_x(e):
@@ -121,11 +124,9 @@ def tile_fakegptossexperts_e_kernel(
             for g in range(PASSES * e, PASSES * e + PASSES):
                 load_words(dn_words, down_proj_words, g, 1)
 
-        for e in range(E):
-            nc.scalar.dma_start(
-                out=bias_bf[:, PASSES * e : PASSES * (e + 1), :],
-                in_=gate_up_proj_bias[e].rearrange("(c p j) -> p c j", c=PASSES, j=SORTS),
-            )
+        nc.scalar.dma_start(
+            out=bias_src[0 : E * PASSES, :], in_=gate_up_proj_bias.rearrange("e (c n) -> (e c) n", c=PASSES)
+        )
         nc.scalar.dma_start(out=bias_rows[0:P:32, :], in_=down_proj_bias)
 
         load_x(0)
@@ -164,8 +165,19 @@ def tile_fakegptossexperts_e_kernel(
         accs = {}
         out_sb = {}
 
+        def turn_gate_up_bias():
+            spreads["gu"] = psum_tr.tile([P, SORTS, E * PASSES], F32, tag="tr", name="bias_ps")
+            for j in range(SORTS):
+                nc.tensor.matmul(
+                    spreads["gu"][:, j, :],
+                    lhsT=bias_src[:, j:HALF:SORTS],
+                    rhs=ident_bf[:, 0 : E * PASSES],
+                    start=True,
+                    stop=True,
+                )
+
         def prepare_gate_up_bias():
-            pairs = bias_bf[:].rearrange("p k (t s) -> p k t s", s=2)
+            pairs = spreads["gu"][:].rearrange("p (t s) k -> p k t s", s=2)
             nc.scalar.copy(out=bias_gu[:, :, :, 0], in_=pairs[:, :, :, 0])
             nc.scalar.activation(out=bias_gu[:, :, :, 1], in_=pairs[:, :, :, 1], func=ACT.Copy, bias=1.0)
 
@@ -320,10 +332,12 @@ def tile_fakegptossexperts_e_kernel(
             )
             nc.sync.dma_start(out=out[e, m * P : (m + 1) * P, n_cols], in_=out_sb[unit][:, n_cols])
 
+        transpose_x((0, 0))
+        group_x((0, 0))
+        turn_gate_up_bias()
+        transpose_x((0, 1))
+        group_x((0, 1))
         prepare_gate_up_bias()
-        for m in range(TOKEN_TILES):
-            transpose_x((0, m))
-            group_x((0, m))
         sort_planes(0, 0)
         sort_words(rounds[0], 0)
         quantise_x(0)

import math
from contextlib import ExitStack

import concourse.mybir as mybir
from concourse.masks import make_identity

F32 = mybir.dt.float32
BF16 = mybir.dt.bfloat16
I32 = mybir.dt.int32
U32 = mybir.dt.uint32
U8 = mybir.dt.uint8
FP8X4 = mybir.dt.float8_e4m3fn_x4
ALU = mybir.AluOpType
ACT = mybir.ActivationFunctionType

E, T, H, I = 4, 256, 1024, 1024
P = 128
K_PASS = 512
BANK = 512
TOKEN_TILES = T // P
PASSES = H // K_PASS
PLANES = 4
SORTS = 8
HALF = 2 * K_PASS
LIMIT = 7.0
ALPHA = 1.702
GLU_AT_LIMIT = LIMIT / (1.0 + math.exp(-ALPHA * LIMIT))

FLOPS = 2 * E * T * H * 2 * I + 2 * E * T * I * H


def load_scale_planes(nc, planes, scales, first_group):
    for quadrant in range(4):
        nc.sync.dma_start(
            out=planes[32 * quadrant : 32 * quadrant + 4 * PLANES, :].bitcast(I32),
            in_=scales[
                first_group : first_group + PLANES, 4 * quadrant : 4 * quadrant + 4, :
            ].bitcast(I32),
        )


def tile_fakegptossexperts_e_kernel(
    tc,
    x,
    gate_up_proj_words,
    gate_up_proj_scales,
    gate_up_proj_bias,
    down_proj_words,
    down_proj_scales,
    down_proj_bias,
    out,
):
    nc = tc.nc
    groups = E * PASSES
    rounds = [(e, c) for e in range(E) for c in range(PASSES)]
    units = [(e, m) for e in range(E) for m in range(TOKEN_TILES)]
    with ExitStack() as ctx:
        ctx.enter_context(tc.manual_schedule())
        keep = ctx.enter_context(tc.tile_pool(name="keep", bufs=1))
        sorted_pool = ctx.enter_context(tc.tile_pool(name="sorted_pool", bufs=6))
        per_expert = ctx.enter_context(tc.tile_pool(name="per_expert", bufs=2))
        per_round = ctx.enter_context(tc.tile_pool(name="per_round", bufs=2))
        results = ctx.enter_context(tc.tile_pool(name="results", bufs=4))
        psum_mx = ctx.enter_context(tc.psum_pool(name="psum_mx", bufs=6))
        psum_tr = ctx.enter_context(tc.psum_pool(name="psum_tr", bufs=2))

        x_sb = [keep.tile([P, TOKEN_TILES, H], BF16, name="x_sb%d" % e) for e in range(E)]
        gu_raw = [keep.tile([P, 2 * I], U32, name="gu_raw%d" % g, align_bytes=64) for g in range(groups)]
        dn_words = [keep.tile([P, H], U32, name="dn_words%d" % g, align_bytes=64) for g in range(groups)]
        gu_planes_raw = [
            keep.tile([P, 2 * I], U8, name="gu_planes_raw%d" % t, align_bytes=64) for t in range(groups // PLANES)
        ]
        gu_planes = [
            keep.tile([P, 2 * I], U8, name="gu_planes%d" % t, align_bytes=64) for t in range(groups // PLANES)
        ]
        dn_planes = [
            keep.tile([P, H], U8, name="dn_planes%d" % t, align_bytes=64) for t in range(groups // PLANES)
        ]
        bias_rows = keep.tile([P, H], BF16, name="bias_rows")
        pick_expert = keep.tile([P, E, P], BF16, name="pick_expert")
        ident = keep.tile([P, P], F32, name="ident")
        bias_src = keep.tile([P, HALF], BF16, name="bias_src")
        ident_bf = keep.tile([P, P], BF16, name="ident_bf")
        bias_gu = keep.tile([P, E * PASSES, SORTS // 2, 2], F32, name="bias_gu")
        warm = keep.tile([P, 2], F32, name="warm")

        nc.vector.memset(warm[:], 0.0)
        nc.vector.memset(bias_src[:].bitcast(I32), 0)
        nc.vector.memset(gu_planes_raw[0][:].bitcast(I32), 0)
        nc.vector.memset(bias_rows[:].bitcast(I32), 0)
        nc.vector.memset(pick_expert[:].bitcast(I32), 0)
        for e in range(E):
            nc.vector.memset(pick_expert[32 * e : 32 * e + 32, e, :], 1.0)
        nc.vector.memset(gu_planes_raw[1][:].bitcast(I32), 0)
        nc.vector.memset(dn_planes[0][:].bitcast(I32), 0)
        nc.vector.memset(dn_planes[1][:].bitcast(I32), 0)
        make_identity(nc, ident[:])
        make_identity(nc, ident_bf[:])
        nc.scalar.activation(out=warm[:, 1:2], in_=warm[:, 0:1], func=ACT.Gelu_apprx_sigmoid)

        def load_x(e):
            for m in range(TOKEN_TILES):
                nc.sync.dma_start(out=x_sb[e][:, m, :], in_=x[e, m * P : (m + 1) * P, :])

        def load_words(tiles, words, g, pieces):
            width = tiles[g].shape[1] // pieces
            flat = words[g].rearrange("p n t -> p (n t)")
            for piece in range(pieces):
                nc.sync.dma_start(
                    out=tiles[g][:, piece * width : (piece + 1) * width].bitcast(I32),
                    in_=flat[:, 4 * piece * width : 4 * (piece + 1) * width].bitcast(I32),
                )

        def load_gate_up_words(e):
            for c in range(PASSES):
                for g in range(PASSES * e, PASSES * e + PASSES):
                    flat = gate_up_proj_words[g].rearrange("p n t -> p (n t)")
                    nc.sync.dma_start(
                        out=gu_raw[g][:, c * HALF : (c + 1) * HALF].bitcast(I32),
                        in_=flat[:, 4 * c * HALF : 4 * (c + 1) * HALF].bitcast(I32),
                    )

        def load_down_words(e):
            for g in range(PASSES * e, PASSES * e + PASSES):
                load_words(dn_words, down_proj_words, g, 1)

        nc.scalar.dma_start(
            out=bias_src[0 : E * PASSES, :], in_=gate_up_proj_bias.rearrange("e (c n) -> (e c) n", c=PASSES)
        )
        nc.scalar.dma_start(out=bias_rows[0:P:32, :], in_=down_proj_bias)

        load_x(0)
        load_scale_planes(nc, gu_planes_raw[0], gate_up_proj_scales, 0)
        load_gate_up_words(0)
        load_x(1)
        load_gate_up_words(1)
        load_scale_planes(nc, gu_planes_raw[1], gate_up_proj_scales, PLANES)
        load_scale_planes(nc, dn_planes[0], down_proj_scales, 0)
        load_down_words(0)
        load_x(2)
        load_gate_up_words(2)
        load_down_words(1)
        load_x(3)
        load_gate_up_words(3)
        load_scale_planes(nc, dn_planes[1], down_proj_scales, PLANES)
        load_down_words(2)
        load_down_words(3)

        def plane_of(planes, group, cols):
            offset = 4 * (group % PLANES)
            return planes[group // PLANES][offset:P, cols]

        bias_dn = {}
        spreads = {}
        turned = {}
        x_grouped = {}
        x_mx = {}
        gu_sorted = {}
        gus = {}
        glus = {}
        ups = {}
        clipped = {}
        h_grouped = {}
        h_mx = {}
        accs = {}
        out_sb = {}

        def turn_gate_up_bias():
            spreads["gu"] = psum_tr.tile([P, SORTS, E * PASSES], F32, tag="tr", name="bias_ps")
            for j in range(SORTS):
                nc.tensor.matmul(
                    spreads["gu"][:, j, :],
                    lhsT=bias_src[:, j:HALF:SORTS],
                    rhs=ident_bf[:, 0 : E * PASSES],
                    start=True,
                    stop=True,
                )

        def prepare_gate_up_bias():
            pairs = spreads["gu"][:].rearrange("p (t s) k -> p k t s", s=2)
            nc.scalar.copy(out=bias_gu[:, :, :, 0], in_=pairs[:, :, :, 0])
            nc.scalar.activation(out=bias_gu[:, :, :, 1], in_=pairs[:, :, :, 1], func=ACT.Copy, bias=1.0)

        def spread_down_bias(e):
            spreads[e] = psum_tr.tile([P, H], BF16, tag="tr", name="spread_dn")
            for b in range(H // BANK):
                nc.tensor.matmul(
                    spreads[e][:, b * BANK : (b + 1) * BANK],
                    lhsT=pick_expert[:, e, :],
                    rhs=bias_rows[:, b * BANK : (b + 1) * BANK],
                    start=True,
                    stop=True,
                )

        def keep_down_bias(e):
            bias_dn[e] = per_expert.tile([P, H], BF16, name="bias_dn", bufs=3)
            nc.scalar.copy(out=bias_dn[e][:], in_=spreads[e][:])

        def transpose_x(unit):
            e, m = unit
            turned[unit] = psum_tr.tile([P, PASSES, 2, P], F32, tag="tr", name="turned")
            for g in range(PASSES):
                for u in range(2):
                    words = x_sb[e][:, m, :].bitcast(F32)[:, 256 * g + u : 256 * (g + 1) : 2]
                    nc.tensor.transpose(turned[unit][:, g, u, :], words, ident[:])

        def group_x(unit):
            e, m = unit
            if m == 0:
                x_grouped[e] = per_expert.tile([P, PASSES, T, 4], BF16, name="x_grouped", align_bytes=64)
            nc.scalar.copy(
                out=x_grouped[e][:].bitcast(F32)[:, :, m * P : (m + 1) * P, :],
                in_=turned[unit][:].rearrange("p g u r -> p g r u"),
            )

        def quantise_x(e):
            codes = per_expert.tile([P, PASSES, T], U32, name="x_codes", align_bytes=64)
            scales = per_expert.tile([P, PASSES, T], U8, name="x_scales", align_bytes=64)
            nc.vector.quantize_mx(
                out=codes[:].rearrange("p g r -> p (g r)").bitcast(FP8X4),
                scales=scales[:].rearrange("p g r -> p (g r)"),
                in_=x_grouped[e][:].rearrange("p g r t -> p (g r t)"),
            )
            x_mx[e] = (codes, scales)

        def sort_planes(t, c):
            cols = slice(c * HALF, (c + 1) * HALF)
            nc.vector.tensor_copy(
                out=gu_planes[t][:, cols].rearrange("q (a i p) -> q a p i", a=SORTS // 4, i=4),
                in_=gu_planes_raw[t][:, cols].rearrange("q (p a i) -> q a p i", a=SORTS // 4, i=4),
            )

        def sort_words(rnd, g):
            e, c = rnd
            gu_sorted[(rnd, g)] = sorted_pool.tile([P, SORTS, P], U32, name="gu_sorted", align_bytes=64)
            nc.vector.tensor_copy(
                out=gu_sorted[(rnd, g)][:].bitcast(I32).rearrange("q (a i) p -> q a p i", i=4),
                in_=gu_raw[PASSES * e + g][:, c * HALF : (c + 1) * HALF].bitcast(I32).rearrange(
                    "q (p a i) -> q a p i", a=SORTS // 4, i=4
                ),
            )

        def gate_up_matmul(rnd, t):
            e, c = rnd
            codes, scales = x_mx[e]
            gus[(rnd, t)] = psum_mx.tile([P, 2, T], F32, tag="bank", name="gu")
            for s in range(2):
                j = 2 * t + s
                cols = slice(c * HALF + j * P, c * HALF + (j + 1) * P)
                for g in range(PASSES):
                    nc.tensor.matmul_mx(
                        out=gus[(rnd, t)][:, s, :],
                        lhsT=gu_sorted[(rnd, g)][:, j, :].bitcast(FP8X4),
                        lhsT_scale=plane_of(gu_planes, PASSES * e + g, cols),
                        rhs=codes[:, g, :].bitcast(FP8X4),
                        rhs_scale=scales[:, g, :],
                        start=(g == 0),
                        stop=(g == PASSES - 1),
                    )

        def leave_psum(rnd, t):
            e, c = rnd
            if t == 0:
                glus[rnd] = per_round.tile([P, 4, T], F32, name="glu", bufs=3)
                ups[rnd] = per_round.tile([P, 4, T], F32, name="up", bufs=3)
            k = PASSES * e + c
            nc.scalar.activation(
                out=glus[rnd][:, t, :], in_=gus[(rnd, t)][:, 0, :], func=ACT.Gelu_apprx_sigmoid,
                bias=bias_gu[:, k, t, 0:1],
            )
            nc.scalar.activation(
                out=ups[rnd][:, t, :], in_=gus[(rnd, t)][:, 1, :], func=ACT.Identity, bias=bias_gu[:, k, t, 1:2]
            )

        def clamp_up(rnd):
            clipped[rnd] = per_round.tile([P, T, 4], F32, name="clipped")
            nc.vector.tensor_scalar(
                out=clipped[rnd][:].rearrange("q (b i) t -> q b t i", i=4),
                in0=ups[rnd][:].rearrange("q t (b i) -> q b t i", i=4),
                scalar1=1.0 + LIMIT,
                scalar2=1.0 - LIMIT,
                op0=ALU.min,
                op1=ALU.max,
            )

        def gated_product(rnd):
            h_grouped[rnd] = per_round.tile([P, T, 4], BF16, name="h_grouped", align_bytes=64)
            nc.vector.scalar_tensor_tensor(
                out=h_grouped[rnd][:],
                in0=glus[rnd][:].rearrange("q t r -> q r t"),
                scalar=GLU_AT_LIMIT,
                in1=clipped[rnd][:],
                op0=ALU.min,
                op1=ALU.mult,
            )

        def quantise_h(rnd):
            codes = per_round.tile([P, T], U32, name="h_codes", align_bytes=64, bufs=4)
            scales = per_round.tile([P, T], U8, name="h_scales", align_bytes=64, bufs=4)
            nc.vector.quantize_mx(
                out=codes[:].bitcast(FP8X4),
                scales=scales[:],
                in_=h_grouped[rnd][:].rearrange("p r t -> p (r t)"),
            )
            h_mx[rnd] = (codes, scales)

        def down_matmul(unit, b):
            e, m = unit
            accs[(unit, b)] = psum_mx.tile([P, BANK], F32, tag="bank", name="acc")
            n_cols = slice(b * BANK, (b + 1) * BANK)
            tokens = slice(m * P, (m + 1) * P)
            for c in range(PASSES):
                codes, scales = h_mx[(e, c)]
                group = PASSES * e + c
                nc.tensor.matmul_mx(
                    out=accs[(unit, b)][:],
                    lhsT=codes[:, tokens].bitcast(FP8X4),
                    lhsT_scale=scales[:, tokens],
                    rhs=dn_words[group][:, n_cols].bitcast(FP8X4),
                    rhs_scale=plane_of(dn_planes, group, n_cols),
                    start=(c == 0),
                    stop=(c == PASSES - 1),
                )

        def add_down_bias_and_store(unit, b):
            e, m = unit
            if b == 0:
                out_sb[unit] = results.tile([P, H], F32, name="out_sb")
            n_cols = slice(b * BANK, (b + 1) * BANK)
            nc.vector.tensor_tensor(
                out=out_sb[unit][:, n_cols], in0=accs[(unit, b)][:], in1=bias_dn[e][:, n_cols], op=ALU.add
            )
            nc.sync.dma_start(out=out[e, m * P : (m + 1) * P, n_cols], in_=out_sb[unit][:, n_cols])

        transpose_x((0, 0))
        group_x((0, 0))
        turn_gate_up_bias()
        transpose_x((0, 1))
        group_x((0, 1))
        prepare_gate_up_bias()
        sort_planes(0, 0)
        sort_words(rounds[0], 0)
        quantise_x(0)
        sort_words(rounds[0], 1)
        sort_planes(0, 1)

        for i in range(len(rounds) + 3):
            rnd = rounds[i] if i < len(rounds) else None
            ahead = rounds[i + 1] if i + 1 < len(rounds) else None
            behind = rounds[i - 1] if 1 <= i <= len(rounds) else None
            out_unit = units[i - 3] if 0 <= i - 3 < len(units) else None
            e, c = divmod(i, PASSES)
            next_x = e + 1 if rnd and e + 1 < E else None
            if behind:
                clamp_up(behind)
            if rnd:
                for t in range(2):
                    gate_up_matmul(rnd, t)
                    leave_psum(rnd, t)
            if ahead:
                sort_words(ahead, 0)
            if behind:
                gated_product(behind)
            if ahead:
                sort_words(ahead, 1)
            if behind:
                quantise_h(behind)
            if next_x and c == 1:
                quantise_x(next_x)
            if rnd:
                for t in range(2, 4):
                    gate_up_matmul(rnd, t)
                    leave_psum(rnd, t)
            if out_unit:
                down_matmul(out_unit, 0)
                down_matmul(out_unit, 1)
            if next_x and c == 0:
                for m in range(TOKEN_TILES):
                    transpose_x((next_x, m))
                    group_x((next_x, m))
            if rnd and c == 0:
                spread_down_bias(e)
                keep_down_bias(e)
            if out_unit:
                add_down_bias_and_store(out_unit, 0)
                add_down_bias_and_store(out_unit, 1)
            if i == 2:
                sort_planes(1, 0)
                sort_planes(1, 1)
